import numpy as np
import ml_dtypes


def mxq(x, axis, fmt="e4m3"):
    dtype, down = {"e4m3": (ml_dtypes.float8_e4m3fn, 7), "e5m2": (ml_dtypes.float8_e5m2, 14)}[fmt]
    v = np.moveaxis(np.asarray(x, np.float32).astype(ml_dtypes.bfloat16).astype(np.float64), axis, -1)
    blocks = v.reshape(v.shape[:-1] + (-1, 32))
    amax = np.abs(blocks).max(-1, keepdims=True)
    byte = np.maximum(np.where(amax > 0, np.frexp(amax)[1] - 1 + 127, 0) - down, 1)
    scale = np.exp2(byte - 127.0)
    codes = (blocks / scale).astype(np.float32).astype(dtype).astype(np.float64)
    return np.moveaxis((codes * scale).reshape(v.shape), -1, axis)


WIDE = False


def mx_kscale(k):
    if not WIDE:
        return np.ones(k)
    levels = np.array([10, -10, 5, -5, 0])
    a = np.random.permutation(np.resize(levels, k // 512 * 4)).reshape(k // 512, 4)
    idx = np.arange(k)
    return np.exp2(a[idx // 512, idx % 128 // 32])


BF16 = ml_dtypes.bfloat16


def bf(x):
    return np.asarray(x, np.float32).astype(BF16)


def f64(x):
    return np.asarray(x).astype(np.float64)


E2M1 = np.array([0.0, 0.5, 1.0, 1.5, 2.0, 3.0, 4.0, 6.0, -0.0, -0.5, -1.0, -1.5, -2.0, -3.0, -4.0, -6.0])


def pack_weight(w, fmt):
    k, n = w.shape
    w = f64(bf(w)).reshape(k // 32, 32, n)
    amax = np.abs(w).max(1)
    if fmt == "e4m3":
        byte = np.frexp(amax)[1] - 1 + 127 - 7
    else:
        mant, ex = np.frexp(amax / 6.0)
        byte = np.where(mant > 0.5, ex, ex - 1) + 127
    byte = np.clip(np.where(amax > 0, byte, 1), 1, 254)
    scaled = (w * np.exp2(127.0 - byte)[:, None, :]).reshape(k, n).astype(np.float32)
    by_word = np.ascontiguousarray(scaled.reshape(k // 512, 128, 4, n).transpose(0, 1, 3, 2))
    if fmt == "e4m3":
        words = by_word.astype(ml_dtypes.float8_e4m3fn).view(np.uint8)
    else:
        c = by_word.astype(ml_dtypes.float4_e2m1fn).view(np.uint8) & 0xF
        words = c[..., 0::2] | (c[..., 1::2] << 4)
    return np.ascontiguousarray(words), np.ascontiguousarray(byte.astype(np.uint8).reshape(k // 512, 16, n))


def unpack_weight(words, scales, fmt):
    g, p, n, _ = words.shape
    if fmt == "e4m3":
        vals = np.ascontiguousarray(words).view(ml_dtypes.float8_e4m3fn).astype(np.float64)
    else:
        nib = np.empty((g, p, n, 4), np.uint8)
        nib[..., 0::2] = words & 0xF
        nib[..., 1::2] = words >> 4
        vals = E2M1[nib]
    vals = vals * np.repeat(np.exp2(scales.astype(np.float64) - 127.0), 8, axis=1)[..., None]
    return vals.transpose(0, 1, 3, 2).reshape(g * 512, n)


B, S, D, E = 2, 2048, 512, 256
EPS = 1e-5
FMT = "e4m3"


def layer_norm(x, g, b):
    mu = x.mean(-1, keepdims=True)
    var = np.square(x - mu).mean(-1, keepdims=True)
    return (x - mu) / np.sqrt(var + EPS) * g + b


def setup_inputs():
    s = mx_kscale(D)

    def stream():
        return bf(np.random.standard_normal((B, S, D)) + 0.5 * np.random.standard_normal((B, S, 1)))

    def gain():
        return bf((1.0 + 0.1 * np.random.standard_normal(D)) * s)

    def shift():
        return bf(0.1 * np.random.standard_normal(D) * s)

    def weight(a):
        w = np.random.standard_normal((E, D)) * a / np.sqrt(D) / s[None, :]
        return pack_weight(np.ascontiguousarray(w.T), FMT)

    def bias():
        return bf(0.2 * np.random.standard_normal(E))

    text = stream()
    img = stream()
    ln_t_g = gain()
    ln_t_b = shift()
    ln_i_g = gain()
    ln_i_b = shift()
    Wq_words, Wq_scales = weight(1.5)
    bq = bias()
    Wkt_words, Wkt_scales = weight(1.5)
    bkt = bias()
    Wvt_words, Wvt_scales = weight(1.0)
    bvt = bias()
    Wki_words, Wki_scales = weight(1.5)
    bki = bias()
    Wvi_words, Wvi_scales = weight(1.0)
    bvi = bias()
    return {"text": text, "img": img,
            "ln_t_g": ln_t_g, "ln_t_b": ln_t_b, "ln_i_g": ln_i_g, "ln_i_b": ln_i_b,
            "Wq_words": Wq_words, "Wq_scales": Wq_scales, "bq": bq,
            "Wkt_words": Wkt_words, "Wkt_scales": Wkt_scales, "bkt": bkt,
            "Wvt_words": Wvt_words, "Wvt_scales": Wvt_scales, "bvt": bvt,
            "Wki_words": Wki_words, "Wki_scales": Wki_scales, "bki": bki,
            "Wvi_words": Wvi_words, "Wvi_scales": Wvi_scales, "bvi": bvi}


def reference(text, img, ln_t_g, ln_t_b, ln_i_g, ln_i_b, Wq_words, Wq_scales, bq, Wkt_words, Wkt_scales, bkt, Wvt_words, Wvt_scales, bvt, Wki_words, Wki_scales, bki, Wvi_words, Wvi_scales, bvi):
    tn = mxq(layer_norm(f64(text), f64(ln_t_g), f64(ln_t_b)), 2, "e4m3")
    im = mxq(layer_norm(f64(img), f64(ln_i_g), f64(ln_i_b)), 2, "e4m3")
    wq = unpack_weight(Wq_words, Wq_scales, FMT)
    q = np.concatenate([(tn @ wq), (im @ wq)], 0) + f64(bq)
    k = np.concatenate([(tn @ unpack_weight(Wkt_words, Wkt_scales, FMT)) + f64(bkt), (im @ unpack_weight(Wki_words, Wki_scales, FMT)) + f64(bki)], 0)
    v = np.concatenate([(tn @ unpack_weight(Wvt_words, Wvt_scales, FMT)) + f64(bvt), (im @ unpack_weight(Wvi_words, Wvi_scales, FMT)) + f64(bvi)], 0)
    return q, k, v

@@ -1,0 +1,247 @@
+from contextlib import ExitStack
+
+import concourse.mybir as mybir
+from concourse.masks import make_identity
+
+F32 = mybir.dt.float32
+BF16 = mybir.dt.bfloat16
+I32 = mybir.dt.int32
+U32 = mybir.dt.uint32
+U8 = mybir.dt.uint8
+FP8X4 = mybir.dt.float8_e4m3fn_x4
+ACT = mybir.ActivationFunctionType
+ALU = mybir.AluOpType
+
+P = 128
+PACK = 4
+D = P * PACK
+E = 256
+SUB = 4
+QUAD = P * SUB
+TOKENS = 2 * 2048
+QUADS_PER_STREAM = TOKENS // QUAD
+N_QUADS = 2 * QUADS_PER_STREAM
+EPS = 1e-5
+X_AHEAD = 4
+
+FLOPS = 2 * (2 * TOKENS) * D * (3 * E)
+
+
+def tile_modalityadaptivemodule_pa_t_kernel(
+    tc,
+    text, img, ln_t_g, ln_t_b, ln_i_g, ln_i_b,
+    Wq_words, Wq_scales, bq,
+    Wkt_words, Wkt_scales, bkt,
+    Wvt_words, Wvt_scales, bvt,
+    Wki_words, Wki_scales, bki,
+    Wvi_words, Wvi_scales, bvi,
+    out_0, out_1, out_2,
+):
+    nc = tc.nc
+
+    x_dram = [
+        src.flatten_outer_dims().rearrange("(q p i) d -> q p i d", p=P, i=SUB) for src in (text, img)
+    ]
+    out_dram = [
+        dst.flatten_outer_dims().rearrange("(q p i) e -> q p i e", p=P, i=SUB)
+        for dst in (out_0, out_1, out_2)
+    ]
+    weights = [
+        [(Wq_words, Wq_scales), (Wkt_words, Wkt_scales), (Wvt_words, Wvt_scales)],
+        [(Wq_words, Wq_scales), (Wki_words, Wki_scales), (Wvi_words, Wvi_scales)],
+    ]
+    ln_gain = [ln_t_g, ln_i_g]
+    ln_shift = [ln_t_b, ln_i_b]
+
+    with ExitStack() as ctx:
+        const = ctx.enter_context(tc.tile_pool(name="const", bufs=1))
+        x_pool = ctx.enter_context(tc.tile_pool(name="x", bufs=1))
+        stat = ctx.enter_context(tc.tile_pool(name="stat", bufs=3))
+        xn_pool = ctx.enter_context(tc.tile_pool(name="xn", bufs=3))
+        work = ctx.enter_context(tc.tile_pool(name="work", bufs=2))
+        mx_pool = ctx.enter_context(tc.tile_pool(name="mx", bufs=2))
+        res_pool = ctx.enter_context(tc.tile_pool(name="res", bufs=3))
+        psum_xt = ctx.enter_context(tc.psum_pool(name="psum_xt", bufs=PACK))
+        psum_acc = ctx.enter_context(tc.psum_pool(name="psum_acc", bufs=4))
+
+        w_words = [const.tile([P, 3 * E], U32, name="w_words%d" % s, align_bytes=64) for s in range(2)]
+        w_scales = [const.tile([P, 3 * E], U8, name="w_scales%d" % s, align_bytes=64) for s in range(2)]
+        for s in range(2):
+            nc.vector.memset(w_scales[s][:].bitcast(I32), 0)
+        eps_col = const.tile([P, 1], F32, name="eps_col")
+        nc.vector.memset(eps_col[:], EPS)
+        ident = const.tile([P, P], F32, name="ident")
+        make_identity(nc, ident[:])
+
+        x_sb = {}
+
+        def load_x(q):
+            x_sb[q] = x_pool.tile([P, SUB, D], BF16, name="x%d" % q)
+            nc.sync.dma_start(out=x_sb[q][:], in_=x_dram[q // QUADS_PER_STREAM][q % QUADS_PER_STREAM])
+
+        def load_weights(s):
+            for j, (words, scales) in enumerate(weights[s]):
+                cols = slice(j * E, (j + 1) * E)
+                nc.sync.dma_start(
+                    out=w_words[s][:, cols].bitcast(I32),
+                    in_=words[0].rearrange("p n t -> p (n t)").bitcast(I32),
+                )
+            for j, (words, scales) in enumerate(weights[s]):
+                cols = slice(j * E, (j + 1) * E)
+                for quadrant in range(4):
+                    nc.sync.dma_start(
+                        out=w_scales[s][32 * quadrant : 32 * quadrant + 4, cols].bitcast(I32),
+                        in_=scales[0, 4 * quadrant : 4 * quadrant + 4, :].bitcast(I32),
+                    )
+
+        for q in range(X_AHEAD):
+            load_x(q)
+        load_weights(0)
+        for q in range(X_AHEAD, QUADS_PER_STREAM):
+            load_x(q)
+        load_weights(1)
+        for q in range(QUADS_PER_STREAM, N_QUADS):
+            load_x(q)
+
+        g_col = []
+        b_col = []
+        for s in range(2):
+            for vec, cols, label in ((ln_gain[s], g_col, "g"), (ln_shift[s], b_col, "b")):
+                raw = const.tile([P, PACK], BF16, name="ln_%s_bf%d" % (label, s))
+                nc.scalar.dma_start(out=raw[:], in_=vec.rearrange("(c t) -> c t", t=PACK))
+                col = const.tile([P, PACK], F32, name="ln_%s%d" % (label, s))
+                nc.vector.tensor_copy(out=col[:], in_=raw[:])
+                cols.append(col)
+
+        bias_bf = const.tile([P, 5, E], BF16, name="bias_bf")
+        for j, vec in enumerate((bq, bkt, bvt, bki, bvi)):
+            nc.scalar.dma_start(out=bias_bf[:, j, :], in_=vec.partition_broadcast(P))
+        bias_qk = []
+        bias_vv = []
+        for s in range(2):
+            qk = const.tile([P, 2, E], F32, name="bias_qk%d" % s)
+            nc.vector.tensor_copy(out=qk[:, 0, :], in_=bias_bf[:, 0, :])
+            nc.vector.tensor_copy(out=qk[:, 1, :], in_=bias_bf[:, 1 + 2 * s, :])
+            bias_qk.append(qk)
+            vv = const.tile([P, 2, E], F32, name="bias_vv%d" % s)
+            nc.vector.tensor_copy(
+                out=vv[:], in_=bias_bf[:, 2 + 2 * s, :].unsqueeze(1).to_broadcast([P, 2, E])
+            )
+            bias_vv.append(vv)
+
+        mean_var = {}
+        rstd = {}
+        xn = {}
+        xt = {}
+        grouped = {}
+
+        def begin_stats(q):
+            partial = stat.tile([P, SUB, 6], F32, name="partial", tag="partial")
+            mean_var[q] = stat.tile([P, SUB, 2], F32, name="mean_var", tag="mean_var")
+            for i in range(SUB):
+                nc.vector.bn_stats(out=partial[:, i, :], in_=x_sb[q][:, i, :])
+            for i in range(SUB):
+                nc.vector.bn_aggr(out=mean_var[q][:, i, :], in_=partial[:, i, :])
+
+        def finish_stats(q):
+            std = stat.tile([P, SUB], F32, name="std", tag="std")
+            nc.scalar.activation(
+                out=std[:], in_=mean_var[q][:, :, 1], func=ACT.Sqrt, bias=eps_col[:, 0:1], scale=1.0
+            )
+            rstd[q] = stat.tile([P, SUB], F32, name="rstd", tag="rstd")
+            nc.vector.reciprocal(out=rstd[q][:], in_=std[:])
+
+        def normalise(q):
+            xn[q] = xn_pool.tile([P, SUB, PACK, P], F32, name="xn", tag="xn")
+            for i in range(SUB):
+                nc.gpsimd.tensor_scalar(
+                    out=xn[q][:, i, :, :],
+                    in0=x_sb[q][:, i, :].rearrange("p (c t) -> p t c", t=PACK),
+                    scalar1=mean_var[q][:, i, 0:1],
+                    scalar2=rstd[q][:, i : i + 1],
+                    op0=ALU.subtract,
+                    op1=ALU.mult,
+                )
+
+        def transpose(q):
+            xt[q] = []
+            for t in range(PACK):
+                bank = psum_xt.tile([P, QUAD], F32, name="xt", tag="xt")
+                for i in range(SUB):
+                    nc.tensor.transpose(
+                        out=bank[:, i * P : (i + 1) * P], in_=xn[q][:, i, t, :], identity=ident[:]
+                    )
+                xt[q].append(bank)
+
+        def scale_shift(q):
+            s = q // QUADS_PER_STREAM
+            planes = work.tile([P, PACK, QUAD], BF16, name="planes", tag="planes")
+            for t in range(PACK):
+                nc.scalar.activation(
+                    out=planes[:, t, :],
+                    in_=xt[q][t][:],
+                    func=ACT.Identity,
+                    scale=g_col[s][:, t : t + 1],
+                    bias=b_col[s][:, t : t + 1],
+                )
+            grouped[q] = work.tile([P, QUAD, PACK], BF16, name="grouped", tag="grouped", align_bytes=64)
+            nc.scalar.copy(
+                out=grouped[q][:].rearrange("p (n i) t -> p n t i", i=4),
+                in_=planes[:].rearrange("p t (n i) -> p n t i", i=4),
+            )
+
+        def project(q):
+            s = q // QUADS_PER_STREAM
+            codes = mx_pool.tile([P, QUAD], U32, name="codes", tag="codes", align_bytes=64)
+            x_scales = mx_pool.tile([P, QUAD], U8, name="x_scales", tag="x_scales", align_bytes=64)
+            nc.vector.quantize_mx(
+                out=codes[:].bitcast(FP8X4),
+                scales=x_scales[:],
+                in_=grouped[q][:].rearrange("p n t -> p (n t)"),
+            )
+            res = res_pool.tile([P, 3, SUB, E], F32, name="res", tag="res")
+            for pair in range(SUB // 2):
+                acc_v = psum_acc.tile([P, 2, E], F32, name="acc_v", tag="acc")
+                for half in range(2):
+                    i = 2 * pair + half
+                    tokens = slice(i * P, (i + 1) * P)
+                    acc_qk = psum_acc.tile([P, 2, E], F32, name="acc_qk", tag="acc")
+                    nc.tensor.matmul_mx(
+                        out=acc_qk[:].rearrange("p a e -> p (a e)"),
+                        lhsT=codes[:, tokens].bitcast(FP8X4),
+                        lhsT_scale=x_scales[:, tokens],
+                        rhs=w_words[s][:, 0 : 2 * E].bitcast(FP8X4),
+                        rhs_scale=w_scales[s][:, 0 : 2 * E],
+                        start=True,
+                        stop=True,
+                    )
+                    nc.tensor.matmul_mx(
+                        out=acc_v[:, half, :],
+                        lhsT=codes[:, tokens].bitcast(FP8X4),
+                        lhsT_scale=x_scales[:, tokens],
+                        rhs=w_words[s][:, 2 * E : 3 * E].bitcast(FP8X4),
+                        rhs_scale=w_scales[s][:, 2 * E : 3 * E],
+                        start=True,
+                        stop=True,
+                    )
+                    nc.vector.tensor_tensor(
+                        out=res[:, 0:2, i, :], in0=acc_qk[:], in1=bias_qk[s][:], op=ALU.add
+                    )
+                v_rows = res[:, 2, 2 * pair : 2 * pair + 2, :]
+                nc.scalar.copy(out=v_rows, in_=acc_v[:])
+                nc.gpsimd.tensor_tensor(out=v_rows, in0=v_rows, in1=bias_vv[s][:], op=ALU.add)
+            for o in range(3):
+                nc.sync.dma_start(out=out_dram[o][q], in_=res[:, o, :, :])
+
+        for step in range(N_QUADS + 3):
+            if step >= 3:
+                project(step - 3)
+            if 1 <= step <= N_QUADS:
+                finish_stats(step - 1)
+            if 2 <= step <= N_QUADS + 1:
+                scale_shift(step - 2)
+            if 1 <= step <= N_QUADS:
+                normalise(step - 1)
+                transpose(step - 1)
+            if step < N_QUADS:
+                begin_stats(step)

@@ -56,7 +56,7 @@ def tile_modalityadaptivemodule_pa_t_kernel(
     with ExitStack() as ctx:
         const = ctx.enter_context(tc.tile_pool(name="const", bufs=1))
         x_pool = ctx.enter_context(tc.tile_pool(name="x", bufs=1))
-        stat = ctx.enter_context(tc.tile_pool(name="stat", bufs=3))
+        stat = ctx.enter_context(tc.tile_pool(name="stat", bufs=N_QUADS))
         xn_pool = ctx.enter_context(tc.tile_pool(name="xn", bufs=3))
         work = ctx.enter_context(tc.tile_pool(name="work", bufs=2))
         mx_pool = ctx.enter_context(tc.tile_pool(name="mx", bufs=2))
@@ -131,6 +131,7 @@ def tile_modalityadaptivemodule_pa_t_kernel(
 
         mean_var = {}
         rstd = {}
+        shift = {}
         xn = {}
         xt = {}
         grouped = {}
@@ -150,6 +151,11 @@ def tile_modalityadaptivemodule_pa_t_kernel(
             )
             rstd[q] = stat.tile([P, SUB], F32, name="rstd", tag="rstd")
             nc.vector.reciprocal(out=rstd[q][:], in_=std[:])
+            shift[q] = stat.tile([P, SUB], F32, name="shift", tag="shift")
+            nc.vector.scalar_tensor_tensor(
+                out=shift[q][:], in0=mean_var[q][:, :, 0], scalar=-1.0, in1=rstd[q][:],
+                op0=ALU.mult, op1=ALU.mult,
+            )
 
         def normalise(q):
             xn[q] = xn_pool.tile([P, SUB, PACK, P], F32, name="xn", tag="xn")
@@ -157,10 +163,10 @@ def tile_modalityadaptivemodule_pa_t_kernel(
                 nc.gpsimd.tensor_scalar(
                     out=xn[q][:, i, :, :],
                     in0=x_sb[q][:, i, :].rearrange("p (c t) -> p t c", t=PACK),
-                    scalar1=mean_var[q][:, i, 0:1],
-                    scalar2=rstd[q][:, i : i + 1],
-                    op0=ALU.subtract,
-                    op1=ALU.mult,
+                    scalar1=rstd[q][:, i : i + 1],
+                    scalar2=shift[q][:, i : i + 1],
+                    op0=ALU.mult,
+                    op1=ALU.add,
                 )
 
         def transpose(q):
@@ -228,8 +234,11 @@ def tile_modalityadaptivemodule_pa_t_kernel(
                         out=res[:, 0:2, i, :], in0=acc_qk[:], in1=bias_qk[s][:], op=ALU.add
                     )
                 v_rows = res[:, 2, 2 * pair : 2 * pair + 2, :]
-                nc.scalar.copy(out=v_rows, in_=acc_v[:])
-                nc.gpsimd.tensor_tensor(out=v_rows, in0=v_rows, in1=bias_vv[s][:], op=ALU.add)
+                if pair == 0:
+                    nc.scalar.copy(out=v_rows, in_=acc_v[:])
+                    nc.gpsimd.tensor_tensor(out=v_rows, in0=v_rows, in1=bias_vv[s][:], op=ALU.add)
+                else:
+                    nc.vector.tensor_tensor(out=v_rows, in0=acc_v[:], in1=bias_vv[s][:], op=ALU.add)
             for o in range(3):
                 nc.sync.dma_start(out=out_dram[o][q], in_=res[:, o, :, :])
 

@@ -56,8 +56,7 @@ def tile_modalityadaptivemodule_pa_t_kernel(
     with ExitStack() as ctx:
         const = ctx.enter_context(tc.tile_pool(name="const", bufs=1))
         x_pool = ctx.enter_context(tc.tile_pool(name="x", bufs=1))
-        stat = ctx.enter_context(tc.tile_pool(name="stat", bufs=N_QUADS))
-        xn_pool = ctx.enter_context(tc.tile_pool(name="xn", bufs=3))
+        xn_pool = ctx.enter_context(tc.tile_pool(name="xn", bufs=2))
         work = ctx.enter_context(tc.tile_pool(name="work", bufs=2))
         mx_pool = ctx.enter_context(tc.tile_pool(name="mx", bufs=2))
         res_pool = ctx.enter_context(tc.tile_pool(name="res", bufs=3))
@@ -103,57 +102,58 @@ def tile_modalityadaptivemodule_pa_t_kernel(
         for q in range(QUADS_PER_STREAM, N_QUADS):
             load_x(q)
 
-        g_col = []
-        b_col = []
+        ln_raw = []
         for s in range(2):
-            for vec, cols, label in ((ln_gain[s], g_col, "g"), (ln_shift[s], b_col, "b")):
-                raw = const.tile([P, PACK], BF16, name="ln_%s_bf%d" % (label, s))
-                nc.scalar.dma_start(out=raw[:], in_=vec.rearrange("(c t) -> c t", t=PACK))
-                col = const.tile([P, PACK], F32, name="ln_%s%d" % (label, s))
-                nc.vector.tensor_copy(out=col[:], in_=raw[:])
-                cols.append(col)
-
-        bias_bf = const.tile([P, 5, E], BF16, name="bias_bf")
+            g_raw = const.tile([P, PACK], BF16, name="g_raw%d" % s)
+            nc.scalar.dma_start(out=g_raw[:], in_=ln_gain[s].rearrange("(c t) -> c t", t=PACK))
+            b_raw = const.tile([P, PACK], BF16, name="b_raw%d" % s)
+            nc.scalar.dma_start(out=b_raw[:], in_=ln_shift[s].rearrange("(c t) -> c t", t=PACK))
+            ln_raw.append((g_raw, b_raw))
+        bias_raw = const.tile([P, 5, E], BF16, name="bias_raw")
         for j, vec in enumerate((bq, bkt, bvt, bki, bvi)):
-            nc.scalar.dma_start(out=bias_bf[:, j, :], in_=vec.partition_broadcast(P))
-        bias_qk = []
-        bias_vv = []
-        for s in range(2):
-            qk = const.tile([P, 2, E], F32, name="bias_qk%d" % s)
-            nc.vector.tensor_copy(out=qk[:, 0, :], in_=bias_bf[:, 0, :])
-            nc.vector.tensor_copy(out=qk[:, 1, :], in_=bias_bf[:, 1 + 2 * s, :])
-            bias_qk.append(qk)
-            vv = const.tile([P, 2, E], F32, name="bias_vv%d" % s)
-            nc.vector.tensor_copy(
-                out=vv[:], in_=bias_bf[:, 2 + 2 * s, :].unsqueeze(1).to_broadcast([P, 2, E])
-            )
-            bias_vv.append(vv)
+            nc.scalar.dma_start(out=bias_raw[:, j, :], in_=vec.partition_broadcast(P))
 
-        mean_var = {}
-        rstd = {}
-        shift = {}
+        g_col = [const.tile([P, PACK], F32, name="g_col%d" % s) for s in range(2)]
+        b_col = [const.tile([P, PACK], F32, name="b_col%d" % s) for s in range(2)]
+        bias_qk = [const.tile([P, 2, E], F32, name="bias_qk%d" % s) for s in range(2)]
+        bias_vv = [const.tile([P, 2, E], F32, name="bias_vv%d" % s) for s in range(2)]
+
+        def prepare_stream(s):
+            nc.vector.tensor_copy(out=g_col[s][:], in_=ln_raw[s][0][:])
+            nc.vector.tensor_copy(out=b_col[s][:], in_=ln_raw[s][1][:])
+            nc.vector.tensor_copy(out=bias_qk[s][:, 0, :], in_=bias_raw[:, 0, :])
+            nc.vector.tensor_copy(out=bias_qk[s][:, 1, :], in_=bias_raw[:, 1 + 2 * s, :])
+            nc.vector.tensor_copy(
+                out=bias_vv[s][:], in_=bias_raw[:, 2 + 2 * s, :].unsqueeze(1).to_broadcast([P, 2, E])
+            )
+
+        partial = const.tile([P, N_QUADS, SUB, 6], F32, name="partial")
+        mean_var = const.tile([P, N_QUADS, SUB, 2], F32, name="mean_var")
+        std = const.tile([P, N_QUADS, SUB], F32, name="std")
+        rstd = const.tile([P, N_QUADS, SUB], F32, name="rstd")
+        shift = const.tile([P, N_QUADS, SUB], F32, name="shift")
         xn = {}
         xt = {}
         grouped = {}
+        codes = {}
+        x_scales = {}
+        acc_qk = {}
+        acc_v = {}
+        res = {}
 
-        def begin_stats(q):
-            partial = stat.tile([P, SUB, 6], F32, name="partial", tag="partial")
-            mean_var[q] = stat.tile([P, SUB, 2], F32, name="mean_var", tag="mean_var")
-            for i in range(SUB):
-                nc.vector.bn_stats(out=partial[:, i, :], in_=x_sb[q][:, i, :])
-            for i in range(SUB):
-                nc.vector.bn_aggr(out=mean_var[q][:, i, :], in_=partial[:, i, :])
+        def stats(q, i):
+            nc.vector.bn_stats(out=partial[:, q, i, :], in_=x_sb[q][:, i, :])
+            nc.vector.bn_aggr(out=mean_var[:, q, i, :], in_=partial[:, q, i, :])
+
+        def root(q):
+            nc.scalar.activation(
+                out=std[:, q, :], in_=mean_var[:, q, :, 1], func=ACT.Sqrt, bias=eps_col[:, 0:1], scale=1.0
+            )
 
         def finish_stats(q):
-            std = stat.tile([P, SUB], F32, name="std", tag="std")
-            nc.scalar.activation(
-                out=std[:], in_=mean_var[q][:, :, 1], func=ACT.Sqrt, bias=eps_col[:, 0:1], scale=1.0
-            )
-            rstd[q] = stat.tile([P, SUB], F32, name="rstd", tag="rstd")
-            nc.vector.reciprocal(out=rstd[q][:], in_=std[:])
-            shift[q] = stat.tile([P, SUB], F32, name="shift", tag="shift")
+            nc.vector.reciprocal(out=rstd[:, q, :], in_=std[:, q, :])
             nc.vector.scalar_tensor_tensor(
-                out=shift[q][:], in0=mean_var[q][:, :, 0], scalar=-1.0, in1=rstd[q][:],
+                out=shift[:, q, :], in0=mean_var[:, q, :, 0], scalar=-1.0, in1=rstd[:, q, :],
                 op0=ALU.mult, op1=ALU.mult,
             )
 
@@ -163,8 +163,8 @@ def tile_modalityadaptivemodule_pa_t_kernel(
                 nc.gpsimd.tensor_scalar(
                     out=xn[q][:, i, :, :],
                     in0=x_sb[q][:, i, :].rearrange("p (c t) -> p t c", t=PACK),
-                    scalar1=rstd[q][:, i : i + 1],
-                    scalar2=shift[q][:, i : i + 1],
+                    scalar1=rstd[:, q, i : i + 1],
+                    scalar2=shift[:, q, i : i + 1],
                     op0=ALU.mult,
                     op1=ALU.add,
                 )
@@ -196,61 +196,83 @@ def tile_modalityadaptivemodule_pa_t_kernel(
                 in_=planes[:].rearrange("p t (n i) -> p n t i", i=4),
             )
 
-        def project(q):
-            s = q // QUADS_PER_STREAM
-            codes = mx_pool.tile([P, QUAD], U32, name="codes", tag="codes", align_bytes=64)
-            x_scales = mx_pool.tile([P, QUAD], U8, name="x_scales", tag="x_scales", align_bytes=64)
+        def quantise(q):
+            codes[q] = mx_pool.tile([P, QUAD], U32, name="codes", tag="codes", align_bytes=64)
+            x_scales[q] = mx_pool.tile([P, QUAD], U8, name="x_scales", tag="x_scales", align_bytes=64)
             nc.vector.quantize_mx(
-                out=codes[:].bitcast(FP8X4),
-                scales=x_scales[:],
+                out=codes[q][:].bitcast(FP8X4),
+                scales=x_scales[q][:],
                 in_=grouped[q][:].rearrange("p n t -> p (n t)"),
             )
-            res = res_pool.tile([P, 3, SUB, E], F32, name="res", tag="res")
-            for pair in range(SUB // 2):
-                acc_v = psum_acc.tile([P, 2, E], F32, name="acc_v", tag="acc")
-                for half in range(2):
-                    i = 2 * pair + half
-                    tokens = slice(i * P, (i + 1) * P)
-                    acc_qk = psum_acc.tile([P, 2, E], F32, name="acc_qk", tag="acc")
-                    nc.tensor.matmul_mx(
-                        out=acc_qk[:].rearrange("p a e -> p (a e)"),
-                        lhsT=codes[:, tokens].bitcast(FP8X4),
-                        lhsT_scale=x_scales[:, tokens],
-                        rhs=w_words[s][:, 0 : 2 * E].bitcast(FP8X4),
-                        rhs_scale=w_scales[s][:, 0 : 2 * E],
-                        start=True,
-                        stop=True,
-                    )
-                    nc.tensor.matmul_mx(
-                        out=acc_v[:, half, :],
-                        lhsT=codes[:, tokens].bitcast(FP8X4),
-                        lhsT_scale=x_scales[:, tokens],
-                        rhs=w_words[s][:, 2 * E : 3 * E].bitcast(FP8X4),
-                        rhs_scale=w_scales[s][:, 2 * E : 3 * E],
-                        start=True,
-                        stop=True,
-                    )
-                    nc.vector.tensor_tensor(
-                        out=res[:, 0:2, i, :], in0=acc_qk[:], in1=bias_qk[s][:], op=ALU.add
-                    )
-                v_rows = res[:, 2, 2 * pair : 2 * pair + 2, :]
-                if pair == 0:
-                    nc.scalar.copy(out=v_rows, in_=acc_v[:])
-                    nc.gpsimd.tensor_tensor(out=v_rows, in0=v_rows, in1=bias_vv[s][:], op=ALU.add)
-                else:
-                    nc.vector.tensor_tensor(out=v_rows, in0=acc_v[:], in1=bias_vv[s][:], op=ALU.add)
-            for o in range(3):
-                nc.sync.dma_start(out=out_dram[o][q], in_=res[:, o, :, :])
+            res[q] = res_pool.tile([P, 3, SUB, E], F32, name="res", tag="res")
 
-        for step in range(N_QUADS + 3):
-            if step >= 3:
-                project(step - 3)
-            if 1 <= step <= N_QUADS:
-                finish_stats(step - 1)
-            if 2 <= step <= N_QUADS + 1:
-                scale_shift(step - 2)
-            if 1 <= step <= N_QUADS:
-                normalise(step - 1)
-                transpose(step - 1)
-            if step < N_QUADS:
-                begin_stats(step)
+        def multiply(q, i):
+            s = q // QUADS_PER_STREAM
+            tokens = slice(i * P, (i + 1) * P)
+            if i % 2 == 0:
+                acc_v[q] = psum_acc.tile([P, 2, E], F32, name="acc_v", tag="acc")
+            acc_qk[q] = psum_acc.tile([P, 2, E], F32, name="acc_qk", tag="acc")
+            nc.tensor.matmul_mx(
+                out=acc_qk[q][:].rearrange("p a e -> p (a e)"),
+                lhsT=codes[q][:, tokens].bitcast(FP8X4),
+                lhsT_scale=x_scales[q][:, tokens],
+                rhs=w_words[s][:, 0 : 2 * E].bitcast(FP8X4),
+                rhs_scale=w_scales[s][:, 0 : 2 * E],
+                start=True,
+                stop=True,
+            )
+            nc.tensor.matmul_mx(
+                out=acc_v[q][:, i % 2, :],
+                lhsT=codes[q][:, tokens].bitcast(FP8X4),
+                lhsT_scale=x_scales[q][:, tokens],
+                rhs=w_words[s][:, 2 * E : 3 * E].bitcast(FP8X4),
+                rhs_scale=w_scales[s][:, 2 * E : 3 * E],
+                start=True,
+                stop=True,
+            )
+            return acc_qk[q], acc_v[q]
+
+        def add_bias(q, i, banks):
+            s = q // QUADS_PER_STREAM
+            bank_qk, bank_v = banks
+            nc.vector.tensor_tensor(out=res[q][:, 0:2, i, :], in0=bank_qk[:], in1=bias_qk[s][:], op=ALU.add)
+            if i % 2 == 1:
+                v_rows = res[q][:, 2, i - 1 : i + 1, :]
+                nc.scalar.copy(out=v_rows, in_=bank_v[:])
+                nc.gpsimd.tensor_tensor(out=v_rows, in0=v_rows, in1=bias_vv[s][:], op=ALU.add)
+
+        def store(q):
+            for o in range(3):
+                nc.sync.dma_start(out=out_dram[o][q], in_=res[q][:, o, :, :])
+
+        def live(q):
+            return 0 <= q < N_QUADS
+
+        with tc.manual_schedule():
+            for step in range(N_QUADS + 3):
+                q_stats, q_norm, q_shift, q_proj = step, step - 1, step - 2, step - 3
+                if live(q_norm):
+                    root(q_norm)
+                if live(q_proj):
+                    quantise(q_proj)
+                if live(q_norm):
+                    finish_stats(q_norm)
+                    normalise(q_norm)
+                if live(q_shift):
+                    scale_shift(q_shift)
+                banks = {}
+                if live(q_proj):
+                    banks[0] = multiply(q_proj, 0)
+                for i in range(SUB):
+                    if live(q_proj) and i + 1 < SUB:
+                        banks[i + 1] = multiply(q_proj, i + 1)
+                    if live(q_stats):
+                        stats(q_stats, i)
+                    if live(q_proj):
+                        add_bias(q_proj, i, banks[i])
+                if live(q_norm):
+                    transpose(q_norm)
+                    if q_norm % QUADS_PER_STREAM == 0:
+                        prepare_stream(q_norm // QUADS_PER_STREAM)
+                if live(q_proj):
+                    store(q_proj)

@@ -143,6 +143,8 @@ def tile_modalityadaptivemodule_pa_t_kernel(
 
         def stats(q, i):
             nc.vector.bn_stats(out=partial[:, q, i, :], in_=x_sb[q][:, i, :])
+
+        def aggregate(q, i):
             nc.vector.bn_aggr(out=mean_var[:, q, i, :], in_=partial[:, q, i, :])
 
         def root(q):
@@ -150,8 +152,10 @@ def tile_modalityadaptivemodule_pa_t_kernel(
                 out=std[:, q, :], in_=mean_var[:, q, :, 1], func=ACT.Sqrt, bias=eps_col[:, 0:1], scale=1.0
             )
 
-        def finish_stats(q):
+        def invert(q):
             nc.vector.reciprocal(out=rstd[:, q, :], in_=std[:, q, :])
+
+        def finish_stats(q):
             nc.vector.scalar_tensor_tensor(
                 out=shift[:, q, :], in0=mean_var[:, q, :, 0], scalar=-1.0, in1=rstd[:, q, :],
                 op0=ALU.mult, op1=ALU.mult,
@@ -256,6 +260,10 @@ def tile_modalityadaptivemodule_pa_t_kernel(
                 if live(q_proj):
                     quantise(q_proj)
                 if live(q_norm):
+                    invert(q_norm)
+                if live(q_stats):
+                    stats(q_stats, 0)
+                if live(q_norm):
                     finish_stats(q_norm)
                     normalise(q_norm)
                 if live(q_shift):
@@ -266,10 +274,14 @@ def tile_modalityadaptivemodule_pa_t_kernel(
                 for i in range(SUB):
                     if live(q_proj) and i + 1 < SUB:
                         banks[i + 1] = multiply(q_proj, i + 1)
-                    if live(q_stats):
+                    if live(q_stats) and i > 0:
                         stats(q_stats, i)
                     if live(q_proj):
                         add_bias(q_proj, i, banks[i])
+                    if live(q_stats) and i > 0:
+                        aggregate(q_stats, i - 1)
+                if live(q_stats):
+                    aggregate(q_stats, SUB - 1)
                 if live(q_norm):
                     transpose(q_norm)
                     if q_norm % QUADS_PER_STREAM == 0:

@@ -59,9 +59,10 @@ def tile_modalityadaptivemodule_pa_t_kernel(
         xn_pool = ctx.enter_context(tc.tile_pool(name="xn", bufs=2))
         work = ctx.enter_context(tc.tile_pool(name="work", bufs=2))
         mx_pool = ctx.enter_context(tc.tile_pool(name="mx", bufs=2))
-        res_pool = ctx.enter_context(tc.tile_pool(name="res", bufs=3))
+        res_pool = ctx.enter_context(tc.tile_pool(name="res", bufs=4))
         psum_xt = ctx.enter_context(tc.psum_pool(name="psum_xt", bufs=PACK))
-        psum_acc = ctx.enter_context(tc.psum_pool(name="psum_acc", bufs=4))
+        psum_qk = ctx.enter_context(tc.psum_pool(name="psum_qk", bufs=2))
+        psum_v = ctx.enter_context(tc.psum_pool(name="psum_v", bufs=2))
 
         w_words = [const.tile([P, 3 * E], U32, name="w_words%d" % s, align_bytes=64) for s in range(2)]
         w_scales = [const.tile([P, 3 * E], U8, name="w_scales%d" % s, align_bytes=64) for s in range(2)]
@@ -116,7 +117,7 @@ def tile_modalityadaptivemodule_pa_t_kernel(
         g_col = [const.tile([P, PACK], F32, name="g_col%d" % s) for s in range(2)]
         b_col = [const.tile([P, PACK], F32, name="b_col%d" % s) for s in range(2)]
         bias_qk = [const.tile([P, 2, E], F32, name="bias_qk%d" % s) for s in range(2)]
-        bias_vv = [const.tile([P, 2, E], F32, name="bias_vv%d" % s) for s in range(2)]
+        bias_v = [const.tile([P, SUB, E], F32, name="bias_v%d" % s) for s in range(2)]
 
         def prepare_stream(s):
             nc.vector.tensor_copy(out=g_col[s][:], in_=ln_raw[s][0][:])
@@ -124,12 +125,11 @@ def tile_modalityadaptivemodule_pa_t_kernel(
             nc.vector.tensor_copy(out=bias_qk[s][:, 0, :], in_=bias_raw[:, 0, :])
             nc.vector.tensor_copy(out=bias_qk[s][:, 1, :], in_=bias_raw[:, 1 + 2 * s, :])
             nc.vector.tensor_copy(
-                out=bias_vv[s][:], in_=bias_raw[:, 2 + 2 * s, :].unsqueeze(1).to_broadcast([P, 2, E])
+                out=bias_v[s][:], in_=bias_raw[:, 2 + 2 * s, :].unsqueeze(1).to_broadcast([P, SUB, E])
             )
 
         partial = const.tile([P, N_QUADS, SUB, 6], F32, name="partial")
         mean_var = const.tile([P, N_QUADS, SUB, 2], F32, name="mean_var")
-        std = const.tile([P, N_QUADS, SUB], F32, name="std")
         rstd = const.tile([P, N_QUADS, SUB], F32, name="rstd")
         shift = const.tile([P, N_QUADS, SUB], F32, name="shift")
         xn = {}
@@ -149,11 +149,9 @@ def tile_modalityadaptivemodule_pa_t_kernel(
 
         def root(q):
             nc.scalar.activation(
-                out=std[:, q, :], in_=mean_var[:, q, :, 1], func=ACT.Sqrt, bias=eps_col[:, 0:1], scale=1.0
+                out=rstd[:, q, :], in_=mean_var[:, q, :, 1], func=ACT.Abs_reciprocal_sqrt,
+                bias=eps_col[:, 0:1], scale=1.0,
             )
-
-        def invert(q):
-            nc.vector.reciprocal(out=rstd[:, q, :], in_=std[:, q, :])
 
         def finish_stats(q):
             nc.vector.scalar_tensor_tensor(
@@ -214,8 +212,8 @@ def tile_modalityadaptivemodule_pa_t_kernel(
             s = q // QUADS_PER_STREAM
             tokens = slice(i * P, (i + 1) * P)
             if i % 2 == 0:
-                acc_v[q] = psum_acc.tile([P, 2, E], F32, name="acc_v", tag="acc")
-            acc_qk[q] = psum_acc.tile([P, 2, E], F32, name="acc_qk", tag="acc")
+                acc_v[q] = psum_v.tile([P, 2, E], F32, name="acc_v", tag="acc_v")
+            acc_qk[q] = psum_qk.tile([P, 2, E], F32, name="acc_qk", tag="acc_qk")
             nc.tensor.matmul_mx(
                 out=acc_qk[q][:].rearrange("p a e -> p (a e)"),
                 lhsT=codes[q][:, tokens].bitcast(FP8X4),
@@ -238,53 +236,60 @@ def tile_modalityadaptivemodule_pa_t_kernel(
 
         def add_bias(q, i, banks):
             s = q // QUADS_PER_STREAM
-            bank_qk, bank_v = banks
-            nc.vector.tensor_tensor(out=res[q][:, 0:2, i, :], in0=bank_qk[:], in1=bias_qk[s][:], op=ALU.add)
-            if i % 2 == 1:
-                v_rows = res[q][:, 2, i - 1 : i + 1, :]
-                nc.scalar.copy(out=v_rows, in_=bank_v[:])
-                nc.gpsimd.tensor_tensor(out=v_rows, in0=v_rows, in1=bias_vv[s][:], op=ALU.add)
+            nc.vector.tensor_tensor(out=res[q][:, 0:2, i, :], in0=banks[0][:], in1=bias_qk[s][:], op=ALU.add)
 
-        def store(q):
-            for o in range(3):
+        def copy_v(q, i, banks):
+            nc.scalar.copy(out=res[q][:, 2, i - 1 : i + 1, :], in_=banks[1][:])
+
+        def add_bias_v(q):
+            s = q // QUADS_PER_STREAM
+            nc.gpsimd.tensor_tensor(out=res[q][:, 2, :, :], in0=res[q][:, 2, :, :], in1=bias_v[s][:], op=ALU.add)
+
+        def store(q, outputs):
+            for o in outputs:
                 nc.sync.dma_start(out=out_dram[o][q], in_=res[q][:, o, :, :])
 
         def live(q):
             return 0 <= q < N_QUADS
 
         with tc.manual_schedule():
-            for step in range(N_QUADS + 3):
-                q_stats, q_norm, q_shift, q_proj = step, step - 1, step - 2, step - 3
+            for step in range(N_QUADS + 4):
+                q_stats, q_norm, q_shift, q_proj, q_bias = step, step - 1, step - 2, step - 3, step - 4
                 if live(q_norm):
                     root(q_norm)
                 if live(q_proj):
                     quantise(q_proj)
                 if live(q_norm):
-                    invert(q_norm)
-                if live(q_stats):
-                    stats(q_stats, 0)
-                if live(q_norm):
                     finish_stats(q_norm)
-                    normalise(q_norm)
-                if live(q_shift):
-                    scale_shift(q_shift)
                 banks = {}
                 if live(q_proj):
                     banks[0] = multiply(q_proj, 0)
+                    banks[1] = multiply(q_proj, 1)
+                if live(q_norm):
+                    normalise(q_norm)
+                if live(q_bias):
+                    add_bias_v(q_bias)
                 for i in range(SUB):
-                    if live(q_proj) and i + 1 < SUB:
-                        banks[i + 1] = multiply(q_proj, i + 1)
-                    if live(q_stats) and i > 0:
+                    if live(q_stats):
                         stats(q_stats, i)
                     if live(q_proj):
                         add_bias(q_proj, i, banks[i])
+                        if i + 2 < SUB:
+                            banks[i + 2] = multiply(q_proj, i + 2)
                     if live(q_stats) and i > 0:
                         aggregate(q_stats, i - 1)
                 if live(q_stats):
                     aggregate(q_stats, SUB - 1)
+                if live(q_shift):
+                    scale_shift(q_shift)
+                if live(q_proj):
+                    copy_v(q_proj, 1, banks[1])
+                    copy_v(q_proj, 3, banks[3])
                 if live(q_norm):
                     transpose(q_norm)
                     if q_norm % QUADS_PER_STREAM == 0:
                         prepare_stream(q_norm // QUADS_PER_STREAM)
                 if live(q_proj):
-                    store(q_proj)
+                    store(q_proj, (0, 1))
+                if live(q_bias):
+                    store(q_bias, (2,))

@@ -159,17 +159,17 @@ def tile_modalityadaptivemodule_pa_t_kernel(
                 op0=ALU.mult, op1=ALU.mult,
             )
 
-        def normalise(q):
-            xn[q] = xn_pool.tile([P, SUB, PACK, P], F32, name="xn", tag="xn")
-            for i in range(SUB):
-                nc.gpsimd.tensor_scalar(
-                    out=xn[q][:, i, :, :],
-                    in0=x_sb[q][:, i, :].rearrange("p (c t) -> p t c", t=PACK),
-                    scalar1=rstd[:, q, i : i + 1],
-                    scalar2=shift[:, q, i : i + 1],
-                    op0=ALU.mult,
-                    op1=ALU.add,
-                )
+        def normalise(q, i, engine):
+            if q not in xn:
+                xn[q] = xn_pool.tile([P, SUB, PACK, P], F32, name="xn", tag="xn")
+            engine.tensor_scalar(
+                out=xn[q][:, i, :, :],
+                in0=x_sb[q][:, i, :].rearrange("p (c t) -> p t c", t=PACK),
+                scalar1=rstd[:, q, i : i + 1],
+                scalar2=shift[:, q, i : i + 1],
+                op0=ALU.mult,
+                op1=ALU.add,
+            )
 
         def transpose(q):
             xt[q] = []
@@ -261,12 +261,14 @@ def tile_modalityadaptivemodule_pa_t_kernel(
                     quantise(q_proj)
                 if live(q_norm):
                     finish_stats(q_norm)
+                    normalise(q_norm, SUB - 1, nc.vector)
                 banks = {}
                 if live(q_proj):
                     banks[0] = multiply(q_proj, 0)
                     banks[1] = multiply(q_proj, 1)
                 if live(q_norm):
-                    normalise(q_norm)
+                    for i in range(SUB - 1):
+                        normalise(q_norm, i, nc.gpsimd)
                 if live(q_bias):
                     add_bias_v(q_bias)
                 for i in range(SUB):

@@ -257,10 +257,11 @@ def tile_modalityadaptivemodule_pa_t_kernel(
                 q_stats, q_norm, q_shift, q_proj, q_bias = step, step - 1, step - 2, step - 3, step - 4
                 if live(q_norm):
                     root(q_norm)
+                if live(q_norm):
+                    finish_stats(q_norm)
                 if live(q_proj):
                     quantise(q_proj)
                 if live(q_norm):
-                    finish_stats(q_norm)
                     normalise(q_norm, SUB - 1, nc.vector)
                 banks = {}
                 if live(q_proj):
@@ -271,17 +272,15 @@ def tile_modalityadaptivemodule_pa_t_kernel(
                         normalise(q_norm, i, nc.gpsimd)
                 if live(q_bias):
                     add_bias_v(q_bias)
-                for i in range(SUB):
-                    if live(q_stats):
+                for i in range(SUB + 1):
+                    if live(q_stats) and i < SUB:
                         stats(q_stats, i)
-                    if live(q_proj):
-                        add_bias(q_proj, i, banks[i])
-                        if i + 2 < SUB:
-                            banks[i + 2] = multiply(q_proj, i + 2)
                     if live(q_stats) and i > 0:
                         aggregate(q_stats, i - 1)
-                if live(q_stats):
-                    aggregate(q_stats, SUB - 1)
+                    if live(q_proj) and i > 0:
+                        add_bias(q_proj, i - 1, banks[i - 1])
+                        if i + 1 < SUB:
+                            banks[i + 1] = multiply(q_proj, i + 1)
                 if live(q_shift):
                     scale_shift(q_shift)
                 if live(q_proj):

@@ -17,14 +17,16 @@ PACK = 4
 D = P * PACK
 E = 256
 SUB = 4
-QUAD = P * SUB
-TOKENS = 2 * 2048
-QUADS_PER_STREAM = TOKENS // QUAD
-N_QUADS = 2 * QUADS_PER_STREAM
+SUBS_PER_STREAM = 2 * 2048 // P
+N_SUBS = 2 * SUBS_PER_STREAM
+TILES = (2, 2) + (SUB,) * 14 + (2, 2)
+FIRST = tuple(sum(TILES[:k]) for k in range(len(TILES)))
 EPS = 1e-5
-X_AHEAD = 4
+X_AHEAD = 8
 
-FLOPS = 2 * (2 * TOKENS) * D * (3 * E)
+FLOPS = 2 * (N_SUBS * P) * D * (3 * E)
+
+assert sum(TILES) == N_SUBS and SUBS_PER_STREAM in FIRST
 
 
 def tile_modalityadaptivemodule_pa_t_kernel(
@@ -38,14 +40,16 @@ def tile_modalityadaptivemodule_pa_t_kernel(
     out_0, out_1, out_2,
 ):
     nc = tc.nc
+    n_tiles = len(TILES)
 
-    x_dram = [
-        src.flatten_outer_dims().rearrange("(q p i) d -> q p i d", p=P, i=SUB) for src in (text, img)
-    ]
-    out_dram = [
-        dst.flatten_outer_dims().rearrange("(q p i) e -> q p i e", p=P, i=SUB)
-        for dst in (out_0, out_1, out_2)
-    ]
+    def stream(k):
+        return FIRST[k] // SUBS_PER_STREAM
+
+    def rows(flat, first_sub, n):
+        return flat[first_sub * P : (first_sub + n) * P, :].rearrange("(p i) d -> p i d", i=n)
+
+    x_flat = [text.flatten_outer_dims(), img.flatten_outer_dims()]
+    out_flat = [dst.flatten_outer_dims() for dst in (out_0, out_1, out_2)]
     weights = [
         [(Wq_words, Wq_scales), (Wkt_words, Wkt_scales), (Wvt_words, Wvt_scales)],
         [(Wq_words, Wq_scales), (Wki_words, Wki_scales), (Wvi_words, Wvi_scales)],
@@ -70,14 +74,18 @@ def tile_modalityadaptivemodule_pa_t_kernel(
             nc.vector.memset(w_scales[s][:].bitcast(I32), 0)
         eps_col = const.tile([P, 1], F32, name="eps_col")
         nc.vector.memset(eps_col[:], EPS)
+        warm = const.tile([P, 1], F32, name="warm")
+        nc.scalar.activation(out=warm[:], in_=eps_col[:], func=ACT.Abs_reciprocal_sqrt)
         ident = const.tile([P, P], F32, name="ident")
         make_identity(nc, ident[:])
 
         x_sb = {}
 
-        def load_x(q):
-            x_sb[q] = x_pool.tile([P, SUB, D], BF16, name="x%d" % q)
-            nc.sync.dma_start(out=x_sb[q][:], in_=x_dram[q // QUADS_PER_STREAM][q % QUADS_PER_STREAM])
+        def load_x(k):
+            x_sb[k] = x_pool.tile([P, TILES[k], D], BF16, name="x%d" % k)
+            nc.sync.dma_start(
+                out=x_sb[k][:], in_=rows(x_flat[stream(k)], FIRST[k] % SUBS_PER_STREAM, TILES[k])
+            )
 
         def load_weights(s):
             for j, (words, scales) in enumerate(weights[s]):
@@ -94,203 +102,198 @@ def tile_modalityadaptivemodule_pa_t_kernel(
                         in_=scales[0, 4 * quadrant : 4 * quadrant + 4, :].bitcast(I32),
                     )
 
-        for q in range(X_AHEAD):
-            load_x(q)
-        load_weights(0)
-        for q in range(X_AHEAD, QUADS_PER_STREAM):
-            load_x(q)
-        load_weights(1)
-        for q in range(QUADS_PER_STREAM, N_QUADS):
-            load_x(q)
+        for k in range(n_tiles):
+            if FIRST[k] == X_AHEAD:
+                load_weights(0)
+            if FIRST[k] == SUBS_PER_STREAM:
+                load_weights(1)
+            load_x(k)
 
-        ln_raw = []
+        g_col = []
+        b_col = []
         for s in range(2):
             g_raw = const.tile([P, PACK], BF16, name="g_raw%d" % s)
             nc.scalar.dma_start(out=g_raw[:], in_=ln_gain[s].rearrange("(c t) -> c t", t=PACK))
             b_raw = const.tile([P, PACK], BF16, name="b_raw%d" % s)
             nc.scalar.dma_start(out=b_raw[:], in_=ln_shift[s].rearrange("(c t) -> c t", t=PACK))
-            ln_raw.append((g_raw, b_raw))
-        bias_raw = const.tile([P, 5, E], BF16, name="bias_raw")
-        for j, vec in enumerate((bq, bkt, bvt, bki, bvi)):
-            nc.scalar.dma_start(out=bias_raw[:, j, :], in_=vec.partition_broadcast(P))
+            g_f32 = const.tile([P, PACK], F32, name="g_col%d" % s)
+            nc.gpsimd.tensor_copy(out=g_f32[:], in_=g_raw[:])
+            g_col.append(g_f32)
+            b_col.append(b_raw)
+        bias_sb = const.tile([P, 5, E], BF16, name="bias_sb")
+        for j, vec in enumerate((bq, bkt, bki, bvt, bvi)):
+            nc.scalar.dma_start(out=bias_sb[:, j, :], in_=vec.partition_broadcast(P))
+        bias_qk = [bias_sb[:, 0:2, :], bias_sb[:, 0:3:2, :]]
+        bias_v = [bias_sb[:, 3, :], bias_sb[:, 4, :]]
 
-        g_col = [const.tile([P, PACK], F32, name="g_col%d" % s) for s in range(2)]
-        b_col = [const.tile([P, PACK], F32, name="b_col%d" % s) for s in range(2)]
-        bias_qk = [const.tile([P, 2, E], F32, name="bias_qk%d" % s) for s in range(2)]
-        bias_v = [const.tile([P, SUB, E], F32, name="bias_v%d" % s) for s in range(2)]
-
-        def prepare_stream(s):
-            nc.vector.tensor_copy(out=g_col[s][:], in_=ln_raw[s][0][:])
-            nc.vector.tensor_copy(out=b_col[s][:], in_=ln_raw[s][1][:])
-            nc.vector.tensor_copy(out=bias_qk[s][:, 0, :], in_=bias_raw[:, 0, :])
-            nc.vector.tensor_copy(out=bias_qk[s][:, 1, :], in_=bias_raw[:, 1 + 2 * s, :])
-            nc.vector.tensor_copy(
-                out=bias_v[s][:], in_=bias_raw[:, 2 + 2 * s, :].unsqueeze(1).to_broadcast([P, SUB, E])
-            )
-
-        partial = const.tile([P, N_QUADS, SUB, 6], F32, name="partial")
-        mean_var = const.tile([P, N_QUADS, SUB, 2], F32, name="mean_var")
-        rstd = const.tile([P, N_QUADS, SUB], F32, name="rstd")
-        shift = const.tile([P, N_QUADS, SUB], F32, name="shift")
+        partial = const.tile([P, N_SUBS, 6], F32, name="partial")
+        mean_var = const.tile([P, N_SUBS, 2], F32, name="mean_var")
+        rstd = const.tile([P, N_SUBS], F32, name="rstd")
+        shift = const.tile([P, N_SUBS], F32, name="shift")
         xn = {}
         xt = {}
         grouped = {}
         codes = {}
         x_scales = {}
-        acc_qk = {}
         acc_v = {}
         res = {}
 
-        def stats(q, i):
-            nc.vector.bn_stats(out=partial[:, q, i, :], in_=x_sb[q][:, i, :])
+        def subs(k):
+            return slice(FIRST[k], FIRST[k] + TILES[k])
 
-        def aggregate(q, i):
-            nc.vector.bn_aggr(out=mean_var[:, q, i, :], in_=partial[:, q, i, :])
+        def stats(k, i):
+            nc.vector.bn_stats(out=partial[:, FIRST[k] + i, :], in_=x_sb[k][:, i, :])
 
-        def root(q):
+        def aggregate(k, i):
+            nc.vector.bn_aggr(out=mean_var[:, FIRST[k] + i, :], in_=partial[:, FIRST[k] + i, :])
+
+        def root(k):
             nc.scalar.activation(
-                out=rstd[:, q, :], in_=mean_var[:, q, :, 1], func=ACT.Abs_reciprocal_sqrt,
+                out=rstd[:, subs(k)], in_=mean_var[:, subs(k), 1], func=ACT.Abs_reciprocal_sqrt,
                 bias=eps_col[:, 0:1], scale=1.0,
             )
 
-        def finish_stats(q):
+        def finish_stats(k):
             nc.vector.scalar_tensor_tensor(
-                out=shift[:, q, :], in0=mean_var[:, q, :, 0], scalar=-1.0, in1=rstd[:, q, :],
+                out=shift[:, subs(k)], in0=mean_var[:, subs(k), 0], scalar=-1.0, in1=rstd[:, subs(k)],
                 op0=ALU.mult, op1=ALU.mult,
             )
 
-        def normalise(q, i, engine):
-            if q not in xn:
-                xn[q] = xn_pool.tile([P, SUB, PACK, P], F32, name="xn", tag="xn")
+        def normalise(k, i, engine):
+            if k not in xn:
+                xn[k] = xn_pool.tile([P, SUB, PACK, P], F32, name="xn", tag="xn")
+            a = FIRST[k] + i
             engine.tensor_scalar(
-                out=xn[q][:, i, :, :],
-                in0=x_sb[q][:, i, :].rearrange("p (c t) -> p t c", t=PACK),
-                scalar1=rstd[:, q, i : i + 1],
-                scalar2=shift[:, q, i : i + 1],
+                out=xn[k][:, i, :, :],
+                in0=x_sb[k][:, i, :].rearrange("p (c t) -> p t c", t=PACK),
+                scalar1=rstd[:, a : a + 1],
+                scalar2=shift[:, a : a + 1],
                 op0=ALU.mult,
                 op1=ALU.add,
             )
 
-        def transpose(q):
-            xt[q] = []
+        def transpose(k):
+            xt[k] = []
             for t in range(PACK):
-                bank = psum_xt.tile([P, QUAD], F32, name="xt", tag="xt")
-                for i in range(SUB):
+                bank = psum_xt.tile([P, SUB * P], F32, name="xt", tag="xt")
+                for i in range(TILES[k]):
                     nc.tensor.transpose(
-                        out=bank[:, i * P : (i + 1) * P], in_=xn[q][:, i, t, :], identity=ident[:]
+                        out=bank[:, i * P : (i + 1) * P], in_=xn[k][:, i, t, :], identity=ident[:]
                     )
-                xt[q].append(bank)
+                xt[k].append(bank)
 
-        def scale_shift(q):
-            s = q // QUADS_PER_STREAM
-            planes = work.tile([P, PACK, QUAD], BF16, name="planes", tag="planes")
+        def scale_shift(k):
+            s = stream(k)
+            width = TILES[k] * P
+            planes = work.tile([P, PACK, SUB * P], BF16, name="planes", tag="planes")
             for t in range(PACK):
                 nc.scalar.activation(
-                    out=planes[:, t, :],
-                    in_=xt[q][t][:],
+                    out=planes[:, t, 0:width],
+                    in_=xt[k][t][:, 0:width],
                     func=ACT.Identity,
                     scale=g_col[s][:, t : t + 1],
                     bias=b_col[s][:, t : t + 1],
                 )
-            grouped[q] = work.tile([P, QUAD, PACK], BF16, name="grouped", tag="grouped", align_bytes=64)
+            grouped[k] = work.tile([P, SUB * P, PACK], BF16, name="grouped", tag="grouped", align_bytes=64)
             nc.scalar.copy(
-                out=grouped[q][:].rearrange("p (n i) t -> p n t i", i=4),
-                in_=planes[:].rearrange("p t (n i) -> p n t i", i=4),
+                out=grouped[k][:, 0:width, :].rearrange("p (n i) t -> p n t i", i=4),
+                in_=planes[:, :, 0:width].rearrange("p t (n i) -> p n t i", i=4),
             )
 
-        def quantise(q):
-            codes[q] = mx_pool.tile([P, QUAD], U32, name="codes", tag="codes", align_bytes=64)
-            x_scales[q] = mx_pool.tile([P, QUAD], U8, name="x_scales", tag="x_scales", align_bytes=64)
+        def quantise(k):
+            width = TILES[k] * P
+            codes[k] = mx_pool.tile([P, SUB * P], U32, name="codes", tag="codes", align_bytes=64)
+            x_scales[k] = mx_pool.tile([P, SUB * P], U8, name="x_scales", tag="x_scales", align_bytes=64)
             nc.vector.quantize_mx(
-                out=codes[q][:].bitcast(FP8X4),
-                scales=x_scales[q][:],
-                in_=grouped[q][:].rearrange("p n t -> p (n t)"),
+                out=codes[k][:, 0:width].bitcast(FP8X4),
+                scales=x_scales[k][:, 0:width],
+                in_=grouped[k][:, 0:width, :].rearrange("p n t -> p (n t)"),
             )
-            res[q] = res_pool.tile([P, 3, SUB, E], F32, name="res", tag="res")
+            res[k] = res_pool.tile([P, 3, SUB, E], F32, name="res", tag="res")
 
-        def multiply(q, i):
-            s = q // QUADS_PER_STREAM
+        def multiply(k, i):
+            s = stream(k)
             tokens = slice(i * P, (i + 1) * P)
             if i % 2 == 0:
-                acc_v[q] = psum_v.tile([P, 2, E], F32, name="acc_v", tag="acc_v")
-            acc_qk[q] = psum_qk.tile([P, 2, E], F32, name="acc_qk", tag="acc_qk")
+                acc_v[k] = psum_v.tile([P, 2, E], F32, name="acc_v", tag="acc_v")
+            acc_qk = psum_qk.tile([P, 2, E], F32, name="acc_qk", tag="acc_qk")
             nc.tensor.matmul_mx(
-                out=acc_qk[q][:].rearrange("p a e -> p (a e)"),
-                lhsT=codes[q][:, tokens].bitcast(FP8X4),
-                lhsT_scale=x_scales[q][:, tokens],
+                out=acc_qk[:].rearrange("p a e -> p (a e)"),
+                lhsT=codes[k][:, tokens].bitcast(FP8X4),
+                lhsT_scale=x_scales[k][:, tokens],
                 rhs=w_words[s][:, 0 : 2 * E].bitcast(FP8X4),
                 rhs_scale=w_scales[s][:, 0 : 2 * E],
                 start=True,
                 stop=True,
             )
             nc.tensor.matmul_mx(
-                out=acc_v[q][:, i % 2, :],
-                lhsT=codes[q][:, tokens].bitcast(FP8X4),
-                lhsT_scale=x_scales[q][:, tokens],
+                out=acc_v[k][:, i % 2, :],
+                lhsT=codes[k][:, tokens].bitcast(FP8X4),
+                lhsT_scale=x_scales[k][:, tokens],
                 rhs=w_words[s][:, 2 * E : 3 * E].bitcast(FP8X4),
                 rhs_scale=w_scales[s][:, 2 * E : 3 * E],
                 start=True,
                 stop=True,
             )
-            return acc_qk[q], acc_v[q]
+            return acc_qk, acc_v[k]
 
-        def add_bias(q, i, banks):
-            s = q // QUADS_PER_STREAM
-            nc.vector.tensor_tensor(out=res[q][:, 0:2, i, :], in0=banks[0][:], in1=bias_qk[s][:], op=ALU.add)
+        def add_bias(k, i, banks):
+            nc.vector.tensor_tensor(
+                out=res[k][:, 0:2, i, :], in0=banks[0][:], in1=bias_qk[stream(k)], op=ALU.add
+            )
 
-        def copy_v(q, i, banks):
-            nc.scalar.copy(out=res[q][:, 2, i - 1 : i + 1, :], in_=banks[1][:])
+        def copy_v(k, i, banks):
+            nc.scalar.copy(out=res[k][:, 2, i - 1 : i + 1, :], in_=banks[1][:])
 
-        def add_bias_v(q):
-            s = q // QUADS_PER_STREAM
-            nc.gpsimd.tensor_tensor(out=res[q][:, 2, :, :], in0=res[q][:, 2, :, :], in1=bias_v[s][:], op=ALU.add)
+        def add_bias_v(k):
+            n = TILES[k]
+            nc.gpsimd.tensor_tensor(
+                out=res[k][:, 2, 0:n, :],
+                in0=res[k][:, 2, 0:n, :],
+                in1=bias_v[stream(k)].unsqueeze(1).to_broadcast([P, n, E]),
+                op=ALU.add,
+            )
 
-        def store(q, outputs):
+        def store(k, outputs):
             for o in outputs:
-                nc.sync.dma_start(out=out_dram[o][q], in_=res[q][:, o, :, :])
+                nc.sync.dma_start(out=rows(out_flat[o], FIRST[k], TILES[k]), in_=res[k][:, o, 0 : TILES[k], :])
 
-        def live(q):
-            return 0 <= q < N_QUADS
+        def size(k):
+            return TILES[k] if 0 <= k < n_tiles else 0
 
         with tc.manual_schedule():
-            for step in range(N_QUADS + 4):
-                q_stats, q_norm, q_shift, q_proj, q_bias = step, step - 1, step - 2, step - 3, step - 4
-                if live(q_norm):
-                    root(q_norm)
-                if live(q_norm):
-                    finish_stats(q_norm)
-                if live(q_proj):
-                    quantise(q_proj)
-                if live(q_norm):
-                    normalise(q_norm, SUB - 1, nc.vector)
+            for step in range(n_tiles + 4):
+                k_stats, k_norm, k_shift, k_proj, k_bias = step, step - 1, step - 2, step - 3, step - 4
+                if size(k_norm):
+                    root(k_norm)
+                    finish_stats(k_norm)
+                if size(k_proj):
+                    quantise(k_proj)
+                if size(k_norm):
+                    normalise(k_norm, size(k_norm) - 1, nc.vector)
                 banks = {}
-                if live(q_proj):
-                    banks[0] = multiply(q_proj, 0)
-                    banks[1] = multiply(q_proj, 1)
-                if live(q_norm):
-                    for i in range(SUB - 1):
-                        normalise(q_norm, i, nc.gpsimd)
-                if live(q_bias):
-                    add_bias_v(q_bias)
-                for i in range(SUB + 1):
-                    if live(q_stats) and i < SUB:
-                        stats(q_stats, i)
-                    if live(q_stats) and i > 0:
-                        aggregate(q_stats, i - 1)
-                    if live(q_proj) and i > 0:
-                        add_bias(q_proj, i - 1, banks[i - 1])
-                        if i + 1 < SUB:
-                            banks[i + 1] = multiply(q_proj, i + 1)
-                if live(q_shift):
-                    scale_shift(q_shift)
-                if live(q_proj):
-                    copy_v(q_proj, 1, banks[1])
-                    copy_v(q_proj, 3, banks[3])
-                if live(q_norm):
-                    transpose(q_norm)
-                    if q_norm % QUADS_PER_STREAM == 0:
-                        prepare_stream(q_norm // QUADS_PER_STREAM)
-                if live(q_proj):
-                    store(q_proj, (0, 1))
-                if live(q_bias):
-                    store(q_bias, (2,))
+                for i in range(min(2, size(k_proj))):
+                    banks[i] = multiply(k_proj, i)
+                for i in range(size(k_norm) - 1):
+                    normalise(k_norm, i, nc.gpsimd)
+                if size(k_bias):
+                    add_bias_v(k_bias)
+                for i in range(max(size(k_stats), size(k_proj)) + 1):
+                    if i < size(k_stats):
+                        stats(k_stats, i)
+                    if 0 < i <= size(k_stats):
+                        aggregate(k_stats, i - 1)
+                    if 0 < i <= size(k_proj):
+                        add_bias(k_proj, i - 1, banks[i - 1])
+                        if i + 1 < size(k_proj):
+                            banks[i + 1] = multiply(k_proj, i + 1)
+                if size(k_shift):
+                    scale_shift(k_shift)
+                for i in range(1, size(k_proj), 2):
+                    copy_v(k_proj, i, banks[i])
+                if size(k_norm):
+                    transpose(k_norm)
+                if size(k_bias):
+                    store(k_bias, (2,))
+                if size(k_proj):
+                    store(k_proj, (0, 1))

@@ -22,7 +22,7 @@ N_SUBS = 2 * SUBS_PER_STREAM
 TILES = (2, 2) + (SUB,) * 14 + (2, 2)
 FIRST = tuple(sum(TILES[:k]) for k in range(len(TILES)))
 EPS = 1e-5
-X_AHEAD = 8
+X_AHEAD = 16
 
 FLOPS = 2 * (N_SUBS * P) * D * (3 * E)
 
@@ -74,8 +74,6 @@ def tile_modalityadaptivemodule_pa_t_kernel(
             nc.vector.memset(w_scales[s][:].bitcast(I32), 0)
         eps_col = const.tile([P, 1], F32, name="eps_col")
         nc.vector.memset(eps_col[:], EPS)
-        warm = const.tile([P, 1], F32, name="warm")
-        nc.scalar.activation(out=warm[:], in_=eps_col[:], func=ACT.Abs_reciprocal_sqrt)
         ident = const.tile([P, P], F32, name="ident")
         make_identity(nc, ident[:])
 

@@ -107,20 +107,18 @@ def tile_modalityadaptivemodule_pa_t_kernel(
                 load_weights(1)
             load_x(k)
 
-        g_col = []
-        b_col = []
-        for s in range(2):
-            g_raw = const.tile([P, PACK], BF16, name="g_raw%d" % s)
-            nc.scalar.dma_start(out=g_raw[:], in_=ln_gain[s].rearrange("(c t) -> c t", t=PACK))
-            b_raw = const.tile([P, PACK], BF16, name="b_raw%d" % s)
-            nc.scalar.dma_start(out=b_raw[:], in_=ln_shift[s].rearrange("(c t) -> c t", t=PACK))
-            g_f32 = const.tile([P, PACK], F32, name="g_col%d" % s)
-            nc.gpsimd.tensor_copy(out=g_f32[:], in_=g_raw[:])
-            g_col.append(g_f32)
-            b_col.append(b_raw)
+        g_raw = [const.tile([P, PACK], BF16, name="g_raw%d" % s) for s in range(2)]
+        b_col = [const.tile([P, PACK], BF16, name="b_col%d" % s) for s in range(2)]
+        g_col = [const.tile([P, PACK], F32, name="g_col%d" % s) for s in range(2)]
         bias_sb = const.tile([P, 5, E], BF16, name="bias_sb")
-        for j, vec in enumerate((bq, bkt, bki, bvt, bvi)):
-            nc.scalar.dma_start(out=bias_sb[:, j, :], in_=vec.partition_broadcast(P))
+        warm = const.tile([P, 1], F32, name="warm")
+        with tc.manual_schedule(engines={mybir.EngineType.Activation}):
+            for s in range(2):
+                nc.scalar.dma_start(out=g_raw[s][:], in_=ln_gain[s].rearrange("(c t) -> c t", t=PACK))
+                nc.scalar.dma_start(out=b_col[s][:], in_=ln_shift[s].rearrange("(c t) -> c t", t=PACK))
+            for j, vec in enumerate((bq, bkt, bki, bvt, bvi)):
+                nc.scalar.dma_start(out=bias_sb[:, j, :], in_=vec.partition_broadcast(P))
+            nc.scalar.activation(out=warm[:], in_=eps_col[:], func=ACT.Abs_reciprocal_sqrt)
         bias_qk = [bias_sb[:, 0:2, :], bias_sb[:, 0:3:2, :]]
         bias_v = [bias_sb[:, 3, :], bias_sb[:, 4, :]]
 
@@ -265,6 +263,9 @@ def tile_modalityadaptivemodule_pa_t_kernel(
                 if size(k_norm):
                     root(k_norm)
                     finish_stats(k_norm)
+                if step == 1:
+                    for s in range(2):
+                        nc.scalar.copy(out=g_col[s][:], in_=g_raw[s][:])
                 if size(k_proj):
                     quantise(k_proj)
                 if size(k_norm):

@@ -68,14 +68,32 @@ def tile_modalityadaptivemodule_pa_t_kernel(
         psum_qk = ctx.enter_context(tc.psum_pool(name="psum_qk", bufs=2))
         psum_v = ctx.enter_context(tc.psum_pool(name="psum_v", bufs=2))
 
+        eps_col = const.tile([P, 1], F32, name="eps_col")
+        nc.vector.memset(eps_col[:], EPS)
+        bias_rows = const.tile([P, 5 * E], BF16, name="bias_rows")
+        nc.vector.memset(bias_rows[:], 0.0)
+        ones = const.tile([P, P], BF16, name="ones")
+        nc.vector.memset(ones[:], 1.0)
         w_words = [const.tile([P, 3 * E], U32, name="w_words%d" % s, align_bytes=64) for s in range(2)]
         w_scales = [const.tile([P, 3 * E], U8, name="w_scales%d" % s, align_bytes=64) for s in range(2)]
         for s in range(2):
             nc.vector.memset(w_scales[s][:].bitcast(I32), 0)
-        eps_col = const.tile([P, 1], F32, name="eps_col")
-        nc.vector.memset(eps_col[:], EPS)
         ident = const.tile([P, P], F32, name="ident")
         make_identity(nc, ident[:])
+
+        g_raw = [const.tile([P, PACK], BF16, name="g_raw%d" % s) for s in range(2)]
+        b_col = [const.tile([P, PACK], BF16, name="b_col%d" % s) for s in range(2)]
+        g_col = [const.tile([P, PACK], F32, name="g_col%d" % s) for s in range(2)]
+        bias_sb = const.tile([P, 5, E], BF16, name="bias_sb")
+        warm = const.tile([P, 1], F32, name="warm")
+
+        def load_ln(s, queue):
+            queue.dma_start(out=g_raw[s][:], in_=ln_gain[s].rearrange("(c t) -> c t", t=PACK))
+            queue.dma_start(out=b_col[s][:], in_=ln_shift[s].rearrange("(c t) -> c t", t=PACK))
+
+        with tc.manual_schedule(engines={mybir.EngineType.Activation}):
+            load_ln(0, nc.scalar)
+            nc.scalar.activation(out=warm[:], in_=eps_col[:], func=ACT.Abs_reciprocal_sqrt)
 
         x_sb = {}
 
@@ -101,26 +119,33 @@ def tile_modalityadaptivemodule_pa_t_kernel(
                     )
 
         for k in range(n_tiles):
+            if k == 1:
+                for j, vec in enumerate((bq, bkt, bki, bvt, bvi)):
+                    nc.sync.dma_start(
+                        out=bias_rows[0:1, j * E : (j + 1) * E], in_=vec.rearrange("(o e) -> o e", o=1)
+                    )
             if FIRST[k] == X_AHEAD:
                 load_weights(0)
             if FIRST[k] == SUBS_PER_STREAM:
                 load_weights(1)
+                load_ln(1, nc.sync)
             load_x(k)
 
-        g_raw = [const.tile([P, PACK], BF16, name="g_raw%d" % s) for s in range(2)]
-        b_col = [const.tile([P, PACK], BF16, name="b_col%d" % s) for s in range(2)]
-        g_col = [const.tile([P, PACK], F32, name="g_col%d" % s) for s in range(2)]
-        bias_sb = const.tile([P, 5, E], BF16, name="bias_sb")
-        warm = const.tile([P, 1], F32, name="warm")
-        with tc.manual_schedule(engines={mybir.EngineType.Activation}):
-            for s in range(2):
-                nc.scalar.dma_start(out=g_raw[s][:], in_=ln_gain[s].rearrange("(c t) -> c t", t=PACK))
-                nc.scalar.dma_start(out=b_col[s][:], in_=ln_shift[s].rearrange("(c t) -> c t", t=PACK))
-            for j, vec in enumerate((bq, bkt, bki, bvt, bvi)):
-                nc.scalar.dma_start(out=bias_sb[:, j, :], in_=vec.partition_broadcast(P))
-            nc.scalar.activation(out=warm[:], in_=eps_col[:], func=ACT.Abs_reciprocal_sqrt)
         bias_qk = [bias_sb[:, 0:2, :], bias_sb[:, 0:3:2, :]]
         bias_v = [bias_sb[:, 3, :], bias_sb[:, 4, :]]
+
+        def spread_biases():
+            for first, pool, tag in ((0, psum_qk, "acc_qk"), (2, psum_qk, "acc_qk"), (4, psum_v, "acc_v")):
+                n = min(2, 5 - first)
+                bank = pool.tile([P, 2, E], F32, name=tag, tag=tag)
+                nc.tensor.matmul(
+                    out=bank[:, 0:n, :].rearrange("p a e -> p (a e)"),
+                    lhsT=ones[:],
+                    rhs=bias_rows[:, first * E : (first + n) * E],
+                    start=True,
+                    stop=True,
+                )
+                nc.scalar.copy(out=bias_sb[:, first : first + n, :], in_=bank[:, 0:n, :])
 
         partial = const.tile([P, N_SUBS, 6], F32, name="partial")
         mean_var = const.tile([P, N_SUBS, 2], F32, name="mean_var")
@@ -257,15 +282,26 @@ def tile_modalityadaptivemodule_pa_t_kernel(
         def size(k):
             return TILES[k] if 0 <= k < n_tiles else 0
 
+        def end(k):
+            return FIRST[k] + TILES[k] if k < n_tiles else N_SUBS
+
+        def stats_done(step):
+            return -1 if step < 0 else min(end(step) + min(step, size(step + 1)), N_SUBS)
+
+        all_subs = [(k, i) for k in range(n_tiles) for i in range(TILES[k])]
+
         with tc.manual_schedule():
             for step in range(n_tiles + 4):
-                k_stats, k_norm, k_shift, k_proj, k_bias = step, step - 1, step - 2, step - 3, step - 4
+                k_norm, k_shift, k_proj, k_bias = step - 1, step - 2, step - 3, step - 4
+                stat_subs = all_subs[max(stats_done(step - 1), 0) : stats_done(step)]
+                roots = [k for k in range(n_tiles) if stats_done(step - 1) < end(k) <= stats_done(step)]
                 if size(k_norm):
-                    root(k_norm)
                     finish_stats(k_norm)
                 if step == 1:
-                    for s in range(2):
-                        nc.scalar.copy(out=g_col[s][:], in_=g_raw[s][:])
+                    nc.scalar.copy(out=g_col[0][:], in_=g_raw[0][:])
+                    spread_biases()
+                if size(step) and FIRST[step] == SUBS_PER_STREAM:
+                    nc.scalar.copy(out=g_col[1][:], in_=g_raw[1][:])
                 if size(k_proj):
                     quantise(k_proj)
                 if size(k_norm):
@@ -277,17 +313,19 @@ def tile_modalityadaptivemodule_pa_t_kernel(
                     normalise(k_norm, i, nc.gpsimd)
                 if size(k_bias):
                     add_bias_v(k_bias)
-                for i in range(max(size(k_stats), size(k_proj)) + 1):
-                    if i < size(k_stats):
-                        stats(k_stats, i)
-                    if 0 < i <= size(k_stats):
-                        aggregate(k_stats, i - 1)
+                for i in range(max(len(stat_subs), size(k_proj)) + 1):
+                    if i < len(stat_subs):
+                        stats(stat_subs[i][0], stat_subs[i][1])
+                    if 0 < i <= len(stat_subs):
+                        aggregate(stat_subs[i - 1][0], stat_subs[i - 1][1])
                     if 0 < i <= size(k_proj):
                         add_bias(k_proj, i - 1, banks[i - 1])
                         if i + 1 < size(k_proj):
                             banks[i + 1] = multiply(k_proj, i + 1)
                 if size(k_shift):
                     scale_shift(k_shift)
+                for k in roots:
+                    root(k)
                 for i in range(1, size(k_proj), 2):
                     copy_v(k_proj, i, banks[i])
                 if size(k_norm):

@@ -23,6 +23,7 @@ TILES = (2, 2) + (SUB,) * 14 + (2, 2)
 FIRST = tuple(sum(TILES[:k]) for k in range(len(TILES)))
 EPS = 1e-5
 X_AHEAD = 16
+LEAD = 2
 
 FLOPS = 2 * (N_SUBS * P) * D * (3 * E)
 
@@ -266,8 +267,16 @@ def tile_modalityadaptivemodule_pa_t_kernel(
         def copy_v(k, i, banks):
             nc.scalar.copy(out=res[k][:, 2, i - 1 : i + 1, :], in_=banks[1][:])
 
+        def add_bias_v_late(k, banks):
+            nc.vector.tensor_tensor(
+                out=res[k][:, 2, 2:4, :],
+                in0=banks[1][:],
+                in1=bias_v[stream(k)].unsqueeze(1).to_broadcast([P, 2, E]),
+                op=ALU.add,
+            )
+
         def add_bias_v(k):
-            n = TILES[k]
+            n = 2
             nc.gpsimd.tensor_tensor(
                 out=res[k][:, 2, 0:n, :],
                 in0=res[k][:, 2, 0:n, :],
@@ -286,7 +295,7 @@ def tile_modalityadaptivemodule_pa_t_kernel(
             return FIRST[k] + TILES[k] if k < n_tiles else N_SUBS
 
         def stats_done(step):
-            return -1 if step < 0 else min(end(step) + min(step, size(step + 1)), N_SUBS)
+            return -1 if step < 0 else min(end(step) + min(step, LEAD, size(step + 1)), N_SUBS)
 
         all_subs = [(k, i) for k in range(n_tiles) for i in range(TILES[k])]
 
@@ -294,7 +303,6 @@ def tile_modalityadaptivemodule_pa_t_kernel(
             for step in range(n_tiles + 4):
                 k_norm, k_shift, k_proj, k_bias = step - 1, step - 2, step - 3, step - 4
                 stat_subs = all_subs[max(stats_done(step - 1), 0) : stats_done(step)]
-                roots = [k for k in range(n_tiles) if stats_done(step - 1) < end(k) <= stats_done(step)]
                 if size(k_norm):
                     finish_stats(k_norm)
                 if step == 1:
@@ -322,12 +330,14 @@ def tile_modalityadaptivemodule_pa_t_kernel(
                         add_bias(k_proj, i - 1, banks[i - 1])
                         if i + 1 < size(k_proj):
                             banks[i + 1] = multiply(k_proj, i + 1)
+                if size(k_proj) == SUB:
+                    add_bias_v_late(k_proj, banks[3])
                 if size(k_shift):
                     scale_shift(k_shift)
-                for k in roots:
-                    root(k)
-                for i in range(1, size(k_proj), 2):
-                    copy_v(k_proj, i, banks[i])
+                if size(step):
+                    root(step)
+                if size(k_proj):
+                    copy_v(k_proj, 1, banks[1])
                 if size(k_norm):
                     transpose(k_norm)
                 if size(k_bias):

@@ -312,12 +312,13 @@ def tile_modalityadaptivemodule_pa_t_kernel(
                     nc.scalar.copy(out=g_col[1][:], in_=g_raw[1][:])
                 if size(k_proj):
                     quantise(k_proj)
-                if size(k_norm):
+                on_vector = 1 if size(k_norm) < SUB else 0
+                if size(k_norm) and on_vector:
                     normalise(k_norm, size(k_norm) - 1, nc.vector)
                 banks = {}
                 for i in range(min(2, size(k_proj))):
                     banks[i] = multiply(k_proj, i)
-                for i in range(size(k_norm) - 1):
+                for i in range(size(k_norm) - on_vector):
                     normalise(k_norm, i, nc.gpsimd)
                 if size(k_bias):
                     add_bias_v(k_bias)

@@ -23,6 +23,7 @@ TILES = (2, 2) + (SUB,) * 14 + (2, 2)
 FIRST = tuple(sum(TILES[:k]) for k in range(len(TILES)))
 EPS = 1e-5
 X_AHEAD = 16
+BY_SCALAR = ((1, 0), (1, 1))
 LEAD = 2
 
 FLOPS = 2 * (N_SUBS * P) * D * (3 * E)
@@ -135,6 +136,8 @@ def tile_modalityadaptivemodule_pa_t_kernel(
         bias_qk = [bias_sb[:, 0:2, :], bias_sb[:, 0:3:2, :]]
         bias_v = [bias_sb[:, 3, :], bias_sb[:, 4, :]]
 
+        bias_banks = []
+
         def spread_biases():
             for first, pool, tag in ((0, psum_qk, "acc_qk"), (2, psum_qk, "acc_qk"), (4, psum_v, "acc_v")):
                 n = min(2, 5 - first)
@@ -146,6 +149,10 @@ def tile_modalityadaptivemodule_pa_t_kernel(
                     start=True,
                     stop=True,
                 )
+                bias_banks.append((first, n, bank))
+
+        def keep_biases():
+            for first, n, bank in bias_banks:
                 nc.scalar.copy(out=bias_sb[:, first : first + n, :], in_=bank[:, 0:n, :])
 
         partial = const.tile([P, N_SUBS, 6], F32, name="partial")
@@ -168,6 +175,38 @@ def tile_modalityadaptivemodule_pa_t_kernel(
 
         def aggregate(k, i):
             nc.vector.bn_aggr(out=mean_var[:, FIRST[k] + i, :], in_=partial[:, FIRST[k] + i, :])
+
+        neg_mean = const.tile([P, len(BY_SCALAR)], F32, name="neg_mean")
+        unused = const.tile([P, D], BF16, name="unused")
+
+        def scalar_mean(j):
+            k, i = BY_SCALAR[j]
+            nc.scalar.activation(
+                out=unused[:], in_=x_sb[k][:, i, :], func=ACT.Identity, scale=1.0 / D,
+                accum_out=mean_var[:, FIRST[k] + i, 0:1],
+            )
+
+        def scalar_neg_mean(j, n):
+            k, i = BY_SCALAR[j]
+            nc.scalar.activation(
+                out=neg_mean[:, j : j + n], in_=mean_var[:, FIRST[k] + i : FIRST[k] + i + n, 0], func=ACT.Copy,
+                scale=-(D ** -0.5),
+            )
+
+        def scalar_var(j):
+            k, i = BY_SCALAR[j]
+            nc.scalar.activation(
+                out=unused[:], in_=x_sb[k][:, i, :], func=ACT.Square, scale=D ** -0.5,
+                bias=neg_mean[:, j : j + 1], accum_out=mean_var[:, FIRST[k] + i, 1:2],
+            )
+
+        def scalar_stats_head():
+            scalar_mean(0)
+            root(0)
+            scalar_mean(1)
+            scalar_neg_mean(0, 2)
+            scalar_var(0)
+            scalar_var(1)
 
         def root(k):
             nc.scalar.activation(
@@ -295,14 +334,15 @@ def tile_modalityadaptivemodule_pa_t_kernel(
             return FIRST[k] + TILES[k] if k < n_tiles else N_SUBS
 
         def stats_done(step):
-            return -1 if step < 0 else min(end(step) + min(step, LEAD, size(step + 1)), N_SUBS)
+            lead = 3 if step in (1, 2) else min(step, LEAD, size(step + 1))
+            return -1 if step < 0 else min(end(step) + lead, N_SUBS)
 
         all_subs = [(k, i) for k in range(n_tiles) for i in range(TILES[k])]
 
         with tc.manual_schedule():
             for step in range(n_tiles + 4):
                 k_norm, k_shift, k_proj, k_bias = step - 1, step - 2, step - 3, step - 4
-                stat_subs = all_subs[max(stats_done(step - 1), 0) : stats_done(step)]
+                stat_subs = [a for a in all_subs[max(stats_done(step - 1), 0) : stats_done(step)] if a not in BY_SCALAR]
                 if size(k_norm):
                     finish_stats(k_norm)
                 if step == 1:
@@ -335,8 +375,12 @@ def tile_modalityadaptivemodule_pa_t_kernel(
                     add_bias_v_late(k_proj, banks[3])
                 if size(k_shift):
                     scale_shift(k_shift)
-                if size(step):
+                if step == 0:
+                    scalar_stats_head()
+                elif size(step):
                     root(step)
+                if step == 2:
+                    keep_biases()
                 if size(k_proj):
                     copy_v(k_proj, 1, banks[1])
                 if size(k_norm):

@@ -24,7 +24,7 @@ FIRST = tuple(sum(TILES[:k]) for k in range(len(TILES)))
 EPS = 1e-5
 X_AHEAD = 16
 BY_SCALAR = ((1, 0), (1, 1))
-LEAD = 2
+LEAD = 4
 
 FLOPS = 2 * (N_SUBS * P) * D * (3 * E)
 
@@ -373,11 +373,14 @@ def tile_modalityadaptivemodule_pa_t_kernel(
                             banks[i + 1] = multiply(k_proj, i + 1)
                 if size(k_proj) == SUB:
                     add_bias_v_late(k_proj, banks[3])
+                early = step > 0 and end(step) <= stats_done(step - 1)
+                if size(step) and early:
+                    root(step)
                 if size(k_shift):
                     scale_shift(k_shift)
                 if step == 0:
                     scalar_stats_head()
-                elif size(step):
+                elif size(step) and not early:
                     root(step)
                 if step == 2:
                     keep_biases()

@@ -24,6 +24,7 @@ FIRST = tuple(sum(TILES[:k]) for k in range(len(TILES)))
 EPS = 1e-5
 X_AHEAD = 16
 BY_SCALAR = ((1, 0), (1, 1))
+LATE = 11
 LEAD = 4
 
 FLOPS = 2 * (N_SUBS * P) * D * (3 * E)
@@ -314,8 +315,11 @@ def tile_modalityadaptivemodule_pa_t_kernel(
                 op=ALU.add,
             )
 
+        def v_by_vector(k):
+            return TILES[k] == SUB and (k % 2 == 0 or k >= LATE)
+
         def add_bias_v(k):
-            n = 2
+            n = 2 if v_by_vector(k) else TILES[k]
             nc.gpsimd.tensor_tensor(
                 out=res[k][:, 2, 0:n, :],
                 in0=res[k][:, 2, 0:n, :],
@@ -371,7 +375,7 @@ def tile_modalityadaptivemodule_pa_t_kernel(
                         add_bias(k_proj, i - 1, banks[i - 1])
                         if i + 1 < size(k_proj):
                             banks[i + 1] = multiply(k_proj, i + 1)
-                if size(k_proj) == SUB:
+                if size(k_proj) and v_by_vector(k_proj):
                     add_bias_v_late(k_proj, banks[3])
                 early = step > 0 and end(step) <= stats_done(step - 1)
                 if size(step) and early:
@@ -386,6 +390,8 @@ def tile_modalityadaptivemodule_pa_t_kernel(
                     keep_biases()
                 if size(k_proj):
                     copy_v(k_proj, 1, banks[1])
+                    if size(k_proj) == SUB and not v_by_vector(k_proj):
+                        copy_v(k_proj, 3, banks[3])
                 if size(k_norm):
                     transpose(k_norm)
                 if size(k_bias):

@@ -356,7 +356,8 @@ def tile_modalityadaptivemodule_pa_t_kernel(
                     nc.scalar.copy(out=g_col[1][:], in_=g_raw[1][:])
                 if size(k_proj):
                     quantise(k_proj)
-                on_vector = 1 if size(k_norm) < SUB else 0
+                long_add = size(k_bias) == SUB and not v_by_vector(k_bias)
+                on_vector = 1 if size(k_norm) < SUB or long_add else 0
                 if size(k_norm) and on_vector:
                     normalise(k_norm, size(k_norm) - 1, nc.vector)
                 banks = {}

from contextlib import ExitStack

import concourse.mybir as mybir
from concourse.masks import make_identity

F32 = mybir.dt.float32
BF16 = mybir.dt.bfloat16
I32 = mybir.dt.int32
U32 = mybir.dt.uint32
U8 = mybir.dt.uint8
FP8X4 = mybir.dt.float8_e4m3fn_x4
ACT = mybir.ActivationFunctionType
ALU = mybir.AluOpType

P = 128
PACK = 4
D = P * PACK
E = 256
SUB = 4
SUBS_PER_STREAM = 2 * 2048 // P
N_SUBS = 2 * SUBS_PER_STREAM
TILES = (2, 2) + (SUB,) * 14 + (2, 2)
FIRST = tuple(sum(TILES[:k]) for k in range(len(TILES)))
EPS = 1e-5
X_AHEAD = 16
BY_SCALAR = ((1, 0), (1, 1))
LATE = 11
LEAD = 4

FLOPS = 2 * (N_SUBS * P) * D * (3 * E)

assert sum(TILES) == N_SUBS and SUBS_PER_STREAM in FIRST


def tile_modalityadaptivemodule_pa_t_kernel(
    tc,
    text, img, ln_t_g, ln_t_b, ln_i_g, ln_i_b,
    Wq_words, Wq_scales, bq,
    Wkt_words, Wkt_scales, bkt,
    Wvt_words, Wvt_scales, bvt,
    Wki_words, Wki_scales, bki,
    Wvi_words, Wvi_scales, bvi,
    out_0, out_1, out_2,
):
    nc = tc.nc
    n_tiles = len(TILES)

    def stream(k):
        return FIRST[k] // SUBS_PER_STREAM

    def rows(flat, first_sub, n):
        return flat[first_sub * P : (first_sub + n) * P, :].rearrange("(p i) d -> p i d", i=n)

    x_flat = [text.flatten_outer_dims(), img.flatten_outer_dims()]
    out_flat = [dst.flatten_outer_dims() for dst in (out_0, out_1, out_2)]
    weights = [
        [(Wq_words, Wq_scales), (Wkt_words, Wkt_scales), (Wvt_words, Wvt_scales)],
        [(Wq_words, Wq_scales), (Wki_words, Wki_scales), (Wvi_words, Wvi_scales)],
    ]
    ln_gain = [ln_t_g, ln_i_g]
    ln_shift = [ln_t_b, ln_i_b]

    with ExitStack() as ctx:
        const = ctx.enter_context(tc.tile_pool(name="const", bufs=1))
        x_pool = ctx.enter_context(tc.tile_pool(name="x", bufs=1))
        xn_pool = ctx.enter_context(tc.tile_pool(name="xn", bufs=2))
        work = ctx.enter_context(tc.tile_pool(name="work", bufs=2))
        mx_pool = ctx.enter_context(tc.tile_pool(name="mx", bufs=2))
        res_pool = ctx.enter_context(tc.tile_pool(name="res", bufs=4))
        psum_xt = ctx.enter_context(tc.psum_pool(name="psum_xt", bufs=PACK))
        psum_qk = ctx.enter_context(tc.psum_pool(name="psum_qk", bufs=2))
        psum_v = ctx.enter_context(tc.psum_pool(name="psum_v", bufs=2))

        eps_col = const.tile([P, 1], F32, name="eps_col")
        nc.vector.memset(eps_col[:], EPS)
        bias_rows = const.tile([P, 5 * E], BF16, name="bias_rows")
        nc.vector.memset(bias_rows[:], 0.0)
        ones = const.tile([P, P], BF16, name="ones")
        nc.vector.memset(ones[:], 1.0)
        w_words = [const.tile([P, 3 * E], U32, name="w_words%d" % s, align_bytes=64) for s in range(2)]
        w_scales = [const.tile([P, 3 * E], U8, name="w_scales%d" % s, align_bytes=64) for s in range(2)]
        for s in range(2):
            nc.vector.memset(w_scales[s][:].bitcast(I32), 0)
        ident = const.tile([P, P], F32, name="ident")
        make_identity(nc, ident[:])

        g_raw = [const.tile([P, PACK], BF16, name="g_raw%d" % s) for s in range(2)]
        b_col = [const.tile([P, PACK], BF16, name="b_col%d" % s) for s in range(2)]
        g_col = [const.tile([P, PACK], F32, name="g_col%d" % s) for s in range(2)]
        bias_sb = const.tile([P, 5, E], BF16, name="bias_sb")
        warm = const.tile([P, 1], F32, name="warm")

        def load_ln(s, queue):
            queue.dma_start(out=g_raw[s][:], in_=ln_gain[s].rearrange("(c t) -> c t", t=PACK))
            queue.dma_start(out=b_col[s][:], in_=ln_shift[s].rearrange("(c t) -> c t", t=PACK))

        with tc.manual_schedule(engines={mybir.EngineType.Activation}):
            load_ln(0, nc.scalar)
            nc.scalar.activation(out=warm[:], in_=eps_col[:], func=ACT.Abs_reciprocal_sqrt)

        x_sb = {}

        def load_x(k):
            x_sb[k] = x_pool.tile([P, TILES[k], D], BF16, name="x%d" % k)
            nc.sync.dma_start(
                out=x_sb[k][:], in_=rows(x_flat[stream(k)], FIRST[k] % SUBS_PER_STREAM, TILES[k])
            )

        def load_weights(s):
            for j, (words, scales) in enumerate(weights[s]):
                cols = slice(j * E, (j + 1) * E)
                nc.sync.dma_start(
                    out=w_words[s][:, cols].bitcast(I32),
                    in_=words[0].rearrange("p n t -> p (n t)").bitcast(I32),
                )
            for j, (words, scales) in enumerate(weights[s]):
                cols = slice(j * E, (j + 1) * E)
                for quadrant in range(4):
                    nc.sync.dma_start(
                        out=w_scales[s][32 * quadrant : 32 * quadrant + 4, cols].bitcast(I32),
                        in_=scales[0, 4 * quadrant : 4 * quadrant + 4, :].bitcast(I32),
                    )

        for k in range(n_tiles):
            if k == 1:
                for j, vec in enumerate((bq, bkt, bki, bvt, bvi)):
                    nc.sync.dma_start(
                        out=bias_rows[0:1, j * E : (j + 1) * E], in_=vec.rearrange("(o e) -> o e", o=1)
                    )
            if FIRST[k] == X_AHEAD:
                load_weights(0)
            if FIRST[k] == SUBS_PER_STREAM:
                load_weights(1)
                load_ln(1, nc.sync)
            load_x(k)

        bias_qk = [bias_sb[:, 0:2, :], bias_sb[:, 0:3:2, :]]
        bias_v = [bias_sb[:, 3, :], bias_sb[:, 4, :]]

        bias_banks = []

        def spread_biases():
            for first, pool, tag in ((0, psum_qk, "acc_qk"), (2, psum_qk, "acc_qk"), (4, psum_v, "acc_v")):
                n = min(2, 5 - first)
                bank = pool.tile([P, 2, E], F32, name=tag, tag=tag)
                nc.tensor.matmul(
                    out=bank[:, 0:n, :].rearrange("p a e -> p (a e)"),
                    lhsT=ones[:],
                    rhs=bias_rows[:, first * E : (first + n) * E],
                    start=True,
                    stop=True,
                )
                bias_banks.append((first, n, bank))

        def keep_biases():
            for first, n, bank in bias_banks:
                nc.scalar.copy(out=bias_sb[:, first : first + n, :], in_=bank[:, 0:n, :])

        partial = const.tile([P, N_SUBS, 6], F32, name="partial")
        mean_var = const.tile([P, N_SUBS, 2], F32, name="mean_var")
        rstd = const.tile([P, N_SUBS], F32, name="rstd")
        shift = const.tile([P, N_SUBS], F32, name="shift")
        xn = {}
        xt = {}
        grouped = {}
        codes = {}
        x_scales = {}
        acc_v = {}
        res = {}

        def subs(k):
            return slice(FIRST[k], FIRST[k] + TILES[k])

        def stats(k, i):
            nc.vector.bn_stats(out=partial[:, FIRST[k] + i, :], in_=x_sb[k][:, i, :])

        def aggregate(k, i):
            nc.vector.bn_aggr(out=mean_var[:, FIRST[k] + i, :], in_=partial[:, FIRST[k] + i, :])

        neg_mean = const.tile([P, len(BY_SCALAR)], F32, name="neg_mean")
        unused = const.tile([P, D], BF16, name="unused")

        def scalar_mean(j):
            k, i = BY_SCALAR[j]
            nc.scalar.activation(
                out=unused[:], in_=x_sb[k][:, i, :], func=ACT.Identity, scale=1.0 / D,
                accum_out=mean_var[:, FIRST[k] + i, 0:1],
            )

        def scalar_neg_mean(j, n):
            k, i = BY_SCALAR[j]
            nc.scalar.activation(
                out=neg_mean[:, j : j + n], in_=mean_var[:, FIRST[k] + i : FIRST[k] + i + n, 0], func=ACT.Copy,
                scale=-(D ** -0.5),
            )

        def scalar_var(j):
            k, i = BY_SCALAR[j]
            nc.scalar.activation(
                out=unused[:], in_=x_sb[k][:, i, :], func=ACT.Square, scale=D ** -0.5,
                bias=neg_mean[:, j : j + 1], accum_out=mean_var[:, FIRST[k] + i, 1:2],
            )

        def scalar_stats_head():
            scalar_mean(0)
            root(0)
            scalar_mean(1)
            scalar_neg_mean(0, 2)
            scalar_var(0)
            scalar_var(1)

        def root(k):
            nc.scalar.activation(
                out=rstd[:, subs(k)], in_=mean_var[:, subs(k), 1], func=ACT.Abs_reciprocal_sqrt,
                bias=eps_col[:, 0:1], scale=1.0,
            )

        def finish_stats(k):
            nc.vector.scalar_tensor_tensor(
                out=shift[:, subs(k)], in0=mean_var[:, subs(k), 0], scalar=-1.0, in1=rstd[:, subs(k)],
                op0=ALU.mult, op1=ALU.mult,
            )

        def normalise(k, i, engine):
            if k not in xn:
                xn[k] = xn_pool.tile([P, SUB, PACK, P], F32, name="xn", tag="xn")
            a = FIRST[k] + i
            engine.tensor_scalar(
                out=xn[k][:, i, :, :],
                in0=x_sb[k][:, i, :].rearrange("p (c t) -> p t c", t=PACK),
                scalar1=rstd[:, a : a + 1],
                scalar2=shift[:, a : a + 1],
                op0=ALU.mult,
                op1=ALU.add,
            )

        def transpose(k):
            xt[k] = []
            for t in range(PACK):
                bank = psum_xt.tile([P, SUB * P], F32, name="xt", tag="xt")
                for i in range(TILES[k]):
                    nc.tensor.transpose(
                        out=bank[:, i * P : (i + 1) * P], in_=xn[k][:, i, t, :], identity=ident[:]
                    )
                xt[k].append(bank)

        def scale_shift(k):
            s = stream(k)
            width = TILES[k] * P
            planes = work.tile([P, PACK, SUB * P], BF16, name="planes", tag="planes")
            for t in range(PACK):
                nc.scalar.activation(
                    out=planes[:, t, 0:width],
                    in_=xt[k][t][:, 0:width],
                    func=ACT.Identity,
                    scale=g_col[s][:, t : t + 1],
                    bias=b_col[s][:, t : t + 1],
                )
            grouped[k] = work.tile([P, SUB * P, PACK], BF16, name="grouped", tag="grouped", align_bytes=64)
            nc.scalar.copy(
                out=grouped[k][:, 0:width, :].rearrange("p (n i) t -> p n t i", i=4),
                in_=planes[:, :, 0:width].rearrange("p t (n i) -> p n t i", i=4),
            )

        def quantise(k):
            width = TILES[k] * P
            codes[k] = mx_pool.tile([P, SUB * P], U32, name="codes", tag="codes", align_bytes=64)
            x_scales[k] = mx_pool.tile([P, SUB * P], U8, name="x_scales", tag="x_scales", align_bytes=64)
            nc.vector.quantize_mx(
                out=codes[k][:, 0:width].bitcast(FP8X4),
                scales=x_scales[k][:, 0:width],
                in_=grouped[k][:, 0:width, :].rearrange("p n t -> p (n t)"),
            )
            res[k] = res_pool.tile([P, 3, SUB, E], F32, name="res", tag="res")

        def multiply(k, i):
            s = stream(k)
            tokens = slice(i * P, (i + 1) * P)
            if i % 2 == 0:
                acc_v[k] = psum_v.tile([P, 2, E], F32, name="acc_v", tag="acc_v")
            acc_qk = psum_qk.tile([P, 2, E], F32, name="acc_qk", tag="acc_qk")
            nc.tensor.matmul_mx(
                out=acc_qk[:].rearrange("p a e -> p (a e)"),
                lhsT=codes[k][:, tokens].bitcast(FP8X4),
                lhsT_scale=x_scales[k][:, tokens],
                rhs=w_words[s][:, 0 : 2 * E].bitcast(FP8X4),
                rhs_scale=w_scales[s][:, 0 : 2 * E],
                start=True,
                stop=True,
            )
            nc.tensor.matmul_mx(
                out=acc_v[k][:, i % 2, :],
                lhsT=codes[k][:, tokens].bitcast(FP8X4),
                lhsT_scale=x_scales[k][:, tokens],
                rhs=w_words[s][:, 2 * E : 3 * E].bitcast(FP8X4),
                rhs_scale=w_scales[s][:, 2 * E : 3 * E],
                start=True,
                stop=True,
            )
            return acc_qk, acc_v[k]

        def add_bias(k, i, banks):
            nc.vector.tensor_tensor(
                out=res[k][:, 0:2, i, :], in0=banks[0][:], in1=bias_qk[stream(k)], op=ALU.add
            )

        def copy_v(k, i, banks):
            nc.scalar.copy(out=res[k][:, 2, i - 1 : i + 1, :], in_=banks[1][:])

        def add_bias_v_late(k, banks):
            nc.vector.tensor_tensor(
                out=res[k][:, 2, 2:4, :],
                in0=banks[1][:],
                in1=bias_v[stream(k)].unsqueeze(1).to_broadcast([P, 2, E]),
                op=ALU.add,
            )

        def v_by_vector(k):
            return TILES[k] == SUB and (k % 2 == 0 or k >= LATE)

        def add_bias_v(k):
            n = 2 if v_by_vector(k) else TILES[k]
            nc.gpsimd.tensor_tensor(
                out=res[k][:, 2, 0:n, :],
                in0=res[k][:, 2, 0:n, :],
                in1=bias_v[stream(k)].unsqueeze(1).to_broadcast([P, n, E]),
                op=ALU.add,
            )

        def store(k, outputs):
            for o in outputs:
                nc.sync.dma_start(out=rows(out_flat[o], FIRST[k], TILES[k]), in_=res[k][:, o, 0 : TILES[k], :])

        def size(k):
            return TILES[k] if 0 <= k < n_tiles else 0

        def end(k):
            return FIRST[k] + TILES[k] if k < n_tiles else N_SUBS

        def stats_done(step):
            lead = 3 if step in (1, 2) else min(step, LEAD, size(step + 1))
            return -1 if step < 0 else min(end(step) + lead, N_SUBS)

        all_subs = [(k, i) for k in range(n_tiles) for i in range(TILES[k])]

        with tc.manual_schedule():
            for step in range(n_tiles + 4):
                k_norm, k_shift, k_proj, k_bias = step - 1, step - 2, step - 3, step - 4
                stat_subs = [a for a in all_subs[max(stats_done(step - 1), 0) : stats_done(step)] if a not in BY_SCALAR]
                if size(k_norm):
                    finish_stats(k_norm)
                if step == 1:
                    nc.scalar.copy(out=g_col[0][:], in_=g_raw[0][:])
                    spread_biases()
                if size(step) and FIRST[step] == SUBS_PER_STREAM:
                    nc.scalar.copy(out=g_col[1][:], in_=g_raw[1][:])
                if size(k_proj):
                    quantise(k_proj)
                long_add = size(k_bias) == SUB and not v_by_vector(k_bias)
                on_vector = 1 if size(k_norm) < SUB or long_add else 0
                if size(k_norm) and on_vector:
                    normalise(k_norm, size(k_norm) - 1, nc.vector)
                banks = {}
                for i in range(min(2, size(k_proj))):
                    banks[i] = multiply(k_proj, i)
                for i in range(size(k_norm) - on_vector):
                    normalise(k_norm, i, nc.gpsimd)
                if size(k_bias):
                    add_bias_v(k_bias)
                for i in range(max(len(stat_subs), size(k_proj)) + 1):
                    if i < len(stat_subs):
                        stats(stat_subs[i][0], stat_subs[i][1])
                    if 0 < i <= len(stat_subs):
                        aggregate(stat_subs[i - 1][0], stat_subs[i - 1][1])
                    if 0 < i <= size(k_proj):
                        add_bias(k_proj, i - 1, banks[i - 1])
                        if i + 1 < size(k_proj):
                            banks[i + 1] = multiply(k_proj, i + 1)
                if size(k_proj) and v_by_vector(k_proj):
                    add_bias_v_late(k_proj, banks[3])
                early = step > 0 and end(step) <= stats_done(step - 1)
                if size(step) and early:
                    root(step)
                if size(k_shift):
                    scale_shift(k_shift)
                if step == 0:
                    scalar_stats_head()
                elif size(step) and not early:
                    root(step)
                if step == 2:
                    keep_biases()
                if size(k_proj):
                    copy_v(k_proj, 1, banks[1])
                    if size(k_proj) == SUB and not v_by_vector(k_proj):
                        copy_v(k_proj, 3, banks[3])
                if size(k_norm):
                    transpose(k_norm)
                if size(k_bias):
                    store(k_bias, (2,))
                if size(k_proj):
                    store(k_proj, (0, 1))
